import numpy as np
import ml_dtypes


def mxq(x, axis, fmt="e4m3"):
    dtype, down = {"e4m3": (ml_dtypes.float8_e4m3fn, 7), "e5m2": (ml_dtypes.float8_e5m2, 14)}[fmt]
    v = np.moveaxis(np.asarray(x, np.float32).astype(ml_dtypes.bfloat16).astype(np.float64), axis, -1)
    blocks = v.reshape(v.shape[:-1] + (-1, 32))
    amax = np.abs(blocks).max(-1, keepdims=True)
    byte = np.maximum(np.where(amax > 0, np.frexp(amax)[1] - 1 + 127, 0) - down, 1)
    scale = np.exp2(byte - 127.0)
    codes = (blocks / scale).astype(np.float32).astype(dtype).astype(np.float64)
    return np.moveaxis((codes * scale).reshape(v.shape), -1, axis)


WIDE = False


def mx_kscale(k):
    if not WIDE:
        return np.ones(k)
    levels = np.array([30, -30])
    if k % 512:
        return np.exp2(np.random.permutation(np.resize(levels, k // 32))).repeat(32)
    a = np.empty((k // 512, 16))
    for p in range(k // 512):
        a[p, :8] = np.random.permutation(np.resize(levels, 8))
        for g in range(8):
            far = levels[np.abs(levels - a[p, g]) >= 10]
            a[p, g + 8] = far[np.random.randint(len(far))]
    return np.exp2(a.ravel()).repeat(32)


BF16 = ml_dtypes.bfloat16


def bf(x):
    return np.asarray(x, np.float32).astype(BF16)


def f64(x):
    return np.asarray(x).astype(np.float64)


B, S, DIM, H, NOPE, ROPE_SP, V_SP, KV_RANK = 2, 256, 2048, 16, 64, 128, 128, 512
C = 1.0
QK_SP = NOPE + ROPE_SP


def lift(sp):
    return np.concatenate([np.sqrt((sp * sp).sum(-1, keepdims=True) + C), sp], -1)


def rope(u, cos, sin):
    u1, u2 = u[..., 0::2], u[..., 1::2]
    cos, sin = cos[None, :, None, :], sin[None, :, None, :]
    return np.stack([u1 * cos - u2 * sin, u1 * sin + u2 * cos], -1).reshape(u.shape)


def setup_inputs():
    s = mx_kscale(DIM)
    inv = 1.0 / (10000.0 ** (np.arange(0, ROPE_SP, 2) / ROPE_SP))
    ang = np.arange(S)[:, None] * inv[None, :]
    return {"x": bf(np.random.standard_normal((B, S, DIM)) * s),
            "freqs_cos": bf(np.cos(ang)),
            "freqs_sin": bf(np.sin(ang)),
            "wq_w": bf(np.random.standard_normal((H * QK_SP, DIM)) * 0.3 / np.sqrt(DIM) / s[None, :]),
            "wq_b": bf(np.random.standard_normal(H * QK_SP) * 0.1)}


def reference(x, freqs_cos, freqs_sin, wq_w, wq_b):
    q = (mxq(f64(x), 2, "e5m2") @ mxq(f64(wq_w), 1, "e4m3").T) + f64(wq_b)
    q = q.reshape(B, S, H, QK_SP)
    q_nope, q_pe = q[..., :NOPE], q[..., NOPE:]
    q_pe = rope(q_pe, f64(freqs_cos), f64(freqs_sin))
    return lift(np.concatenate([q_nope, q_pe], -1))

@@ -1,0 +1,350 @@
+from contextlib import ExitStack
+
+import concourse.mybir as mybir
+from concourse.masks import make_identity
+
+F32 = mybir.dt.float32
+BF16 = mybir.dt.bfloat16
+I32 = mybir.dt.int32
+U32 = mybir.dt.uint32
+U8 = mybir.dt.uint8
+E5M2X4 = mybir.dt.float8_e5m2_x4
+E4M3X4 = mybir.dt.float8_e4m3fn_x4
+ALU = mybir.AluOpType
+ACT = mybir.ActivationFunctionType
+
+P = 128
+TOKENS = 512
+DIM = 2048
+HEADS = 16
+NOPE = 64
+ROPE = 128
+QK = NOPE + ROPE
+HEAD_OUT = QK + 1
+OUT_COLS = HEADS * HEAD_OUT
+HALF_COLS = 8 * HEAD_OUT
+
+FLOPS = 2 * TOKENS * HEADS * QK * DIM
+
+CHUNKS = (("P", 0), ("P", 1), ("N", 0), ("P", 2), ("P", 3), ("N", 1))
+N_RUNS = 2 + 2 * len(CHUNKS)
+RAW_BUFS = 6
+HEAD_RUNS = 4
+WARMUP = 6
+UNITS_PER_BANK = 2
+
+
+def tile_lorentzmla_pb_kernel(tc, x, freqs_cos, freqs_sin, wq_w, wq_b, out):
+    nc = tc.nc
+    x_rows = x.flatten_outer_dims()
+    out_rows = out.rearrange("b s h c -> (b s) (h c)")
+    w_pe = wq_w.rearrange("(h r) k -> r h k", r=QK)
+    w_np = wq_w.rearrange("(q a r) k -> a r q k", a=2, r=QK)
+
+    with ExitStack() as ctx:
+        const = ctx.enter_context(tc.tile_pool(name="const", bufs=1))
+        rawp = ctx.enter_context(tc.tile_pool(name="rawp", bufs=RAW_BUFS))
+        grpp = ctx.enter_context(tc.tile_pool(name="grpp", bufs=3))
+        codep = ctx.enter_context(tc.tile_pool(name="codep", bufs=3))
+        tpool = ctx.enter_context(tc.tile_pool(name="tpool", bufs=8))
+        uvp = ctx.enter_context(tc.tile_pool(name="uvp", bufs=4))
+        junkp = ctx.enter_context(tc.tile_pool(name="junkp", bufs=2))
+        ps_tr = ctx.enter_context(tc.psum_pool(name="ps_tr", bufs=4))
+        ps_mx = ctx.enter_context(tc.psum_pool(name="ps_mx", bufs=4))
+        ctx.enter_context(tc.manual_schedule())
+
+        ident = const.tile([P, P], F32, name="ident")
+        perm = const.tile([P, P], F32, name="perm")
+        ones_bf = const.tile([P, P], BF16, name="ones_bf")
+        zrhs = const.tile([P, 512], BF16, name="zrhs")
+        brow = const.tile([P, HEADS * QK], BF16, name="brow")
+        b_bc = const.tile([P, HEADS * QK], F32, name="b_bc")
+        cos_t = const.tile([P, 2, 64], BF16, name="cos_t")
+        sin_t = const.tile([P, 2, 64], BF16, name="sin_t")
+        nsin_t = const.tile([P, 2, 64], BF16, name="nsin_t")
+        one_col = const.tile([P, 1], F32, name="one_col")
+        scr_col = const.tile([P, 1], F32, name="scr_col")
+        xq = const.tile([P, 2, 1024], U32, name="xq", align_bytes=64)
+        xs = const.tile([P, 2, 1024], U8, name="xs", align_bytes=64)
+        ssq_pe = const.tile([P, 4, HEADS], F32, name="ssq_pe")
+        ssq_np = const.tile([P, 4, HEADS], F32, name="ssq_np")
+        tot = const.tile([P, 4, HEADS], F32, name="tot")
+        otiles = []
+        for tt in range(4):
+            o_tile = const.tile([P, OUT_COLS], F32, name="o_tile%d" % tt)
+            otiles.append(o_tile)
+
+        raws = {}
+        groups = {}
+        wcodes = {}
+        wscales = {}
+        units = []
+        unit_pos = [0]
+        squares = []
+        r_done = {}
+        nope_done = {}
+
+        def emit_load(i):
+            raw = rawp.tile([P, 4096], BF16, name="raw", tag="raw")
+            raws[i] = raw
+            if i < 2:
+                nc.sync.dma_start(
+                    out=raw.rearrange("p (t k) -> p t k", t=2),
+                    in_=x_rows[256 * i : 256 * (i + 1), :].rearrange("(t p) k -> p t k", p=P),
+                )
+                return
+            kind, idx = CHUNKS[(i - 2) // 2]
+            hf = (i - 2) % 2
+            cols = slice(1024 * hf, 1024 * (hf + 1))
+            dst = raw.rearrange("p (q k) -> p q k", q=4)
+            if kind == "P":
+                nc.sync.dma_start(out=dst, in_=w_pe[NOPE:QK, 4 * idx : 4 * idx + 4, cols])
+            else:
+                for a in range(2):
+                    nc.sync.dma_start(
+                        out=dst[64 * a : 64 * (a + 1), :, :],
+                        in_=w_np[a, 0:NOPE, 4 * idx : 4 * idx + 4, cols],
+                    )
+
+        def emit_run(i):
+            words = raws[i].bitcast(F32)
+            grp = grpp.tile([P, 1024, 4], BF16, name="grp", tag="grp", align_bytes=64)
+            groups[i] = grp
+            grp_words = grp.bitcast(F32)
+            is_pe = i >= 2 and CHUNKS[(i - 2) // 2][0] == "P"
+            mat = perm if is_pe else ident
+            banks = []
+            for k in range(4):
+                bank = ps_tr.tile([P, 2, 256], F32, name="trb", tag="trb")
+                banks.append(bank)
+                for u in range(2):
+                    for r2 in range(2):
+                        if i < 2:
+                            start = 1024 * r2 + 256 * k + u
+                        else:
+                            start = 512 * (2 * (k % 2) + r2) + 256 * (k // 2) + u
+                        nc.tensor.transpose(
+                            bank[:, u, 128 * r2 : 128 * (r2 + 1)],
+                            words[:, start : start + 255 : 2],
+                            mat[:, :],
+                        )
+            for k in range(4):
+                dst = grp_words[:, 256 * k : 256 * (k + 1), :]
+                src = banks[k].rearrange("p u c -> p c u")
+                if i < HEAD_RUNS and k % 2 == 1:
+                    nc.vector.tensor_copy(out=dst, in_=src)
+                else:
+                    nc.scalar.copy(out=dst, in_=src)
+
+        def emit_quant(i):
+            flat = groups[i].rearrange("p c t -> p (c t)")
+            if i < 2:
+                nc.vector.quantize_mx(out=xq[:, i, :].bitcast(E5M2X4), scales=xs[:, i, :], in_=flat)
+                return
+            c = (i - 2) // 2
+            hf = (i - 2) % 2
+            if hf == 0:
+                wq = codep.tile([P, 2048], U32, name="wq", tag="wq", align_bytes=64)
+                ws = codep.tile([P, 2048], U8, name="ws", tag="ws", align_bytes=64)
+                wcodes[c] = wq
+                wscales[c] = ws
+            cols = slice(1024 * hf, 1024 * (hf + 1))
+            nc.vector.quantize_mx(
+                out=wcodes[c][:, cols].bitcast(E4M3X4), scales=wscales[c][:, cols], in_=flat
+            )
+
+        def emit_dummies(n):
+            bank = ps_mx.tile([P, 512], F32, name="acc", tag="acc")
+            for unused in range(n):
+                nc.tensor.matmul(bank[:, :], lhsT=ones_bf[:, :], rhs=zrhs[:, :], start=True, stop=True)
+
+        def emit_bias(k):
+            bank = ps_mx.tile([P, 512], F32, name="acc", tag="acc")
+            cols = slice(512 * k, 512 * (k + 1))
+            nc.tensor.matmul(bank[:, :], lhsT=ones_bf[:, :], rhs=brow[:, cols], start=True, stop=True)
+            nc.vector.tensor_copy(out=b_bc[:, cols], in_=bank[:, :])
+
+        def emit_mx(c, tt):
+            acc = ps_mx.tile([P, 512], F32, name="acc", tag="acc")
+            pair = tt // 2
+            for g in range(4):
+                xc = slice(256 * g + 128 * (tt % 2), 256 * g + 128 * (tt % 2) + 128)
+                wc = slice(512 * g, 512 * (g + 1))
+                nc.tensor.matmul_mx(
+                    out=acc[:, :],
+                    lhsT=xq[:, pair, xc].bitcast(E5M2X4),
+                    lhsT_scale=xs[:, pair, xc],
+                    rhs=wcodes[c][:, wc].bitcast(E4M3X4),
+                    rhs_scale=wscales[c][:, wc],
+                    start=(g == 0),
+                    stop=(g == 3),
+                )
+            return acc
+
+        def flush_squares():
+            for (src, dst, width) in squares:
+                junk = junkp.tile([P, ROPE], F32, name="junk", tag="junk")
+                nc.scalar.activation(out=junk[:, 0:width], in_=src, func=ACT.Square, accum_out=dst)
+            squares.clear()
+
+        def try_finalize(tt, half):
+            if not nope_done.get((tt, half), False):
+                return
+            if r_done.get((tt, half), 0) < 2:
+                return
+            flush_squares()
+            hs = slice(8 * half, 8 * half + 8)
+            nc.vector.scalar_tensor_tensor(
+                out=tot[:, tt, hs], in0=ssq_pe[:, tt, hs], scalar=1.0, in1=ssq_np[:, tt, hs],
+                op0=ALU.add, op1=ALU.add,
+            )
+            o3 = otiles[tt].rearrange("p (h c) -> p h c", c=HEAD_OUT)
+            nc.scalar.activation(out=o3[:, hs, 0:1], in_=tot[:, tt, hs].unsqueeze(2), func=ACT.Sqrt)
+            base = HALF_COLS * half
+            sb = otiles[tt][:, base : base + 1536].rearrange("p (i w) -> p i w", w=192)
+            hb = out_rows[P * tt : P * (tt + 1), base : base + 1536].rearrange("p (i w) -> p i w", w=192)
+            nc.sync.dma_start(out=hb[:, :, 0:72], in_=sb[:, :, 0:72])
+
+        def evac_nope(acc, half, tt):
+            hs = slice(8 * half, 8 * half + 8)
+            o3 = otiles[tt].rearrange("p (h c) -> p h c", c=HEAD_OUT)
+            b3 = b_bc.rearrange("p (h r) -> p h r", r=QK)
+            nc.vector.tensor_tensor(
+                out=o3[:, hs, 1 : 1 + NOPE],
+                in0=acc.rearrange("p (h n) -> p h n", n=NOPE),
+                in1=b3[:, hs, 0:NOPE],
+                op=ALU.add,
+            )
+            for h in range(8 * half, 8 * half + 8):
+                squares.append((o3[:, h, 1 : 1 + NOPE], ssq_np[:, tt, h : h + 1], NOPE))
+            nope_done[(tt, half)] = True
+            try_finalize(tt, half)
+
+        def evac_pe(acc, quad, tt):
+            t = tpool.tile([P, 512], F32, name="t", tag="t")
+            b3 = b_bc.rearrange("p (h r) -> p h r", r=QK)
+            nc.vector.tensor_tensor(
+                out=t.rearrange("p (h e j) -> p h e j", e=2, j=64),
+                in0=acc.rearrange("p (h e j) -> p h e j", e=2, j=64),
+                in1=b3[:, 4 * quad : 4 * quad + 4, NOPE:QK].rearrange("p h (j e) -> p h e j", e=2),
+                op=ALU.add,
+            )
+            return t
+
+        def rope_units(t, quad, tt):
+            st = tt % 2
+            hold = {}
+
+            def unit_u():
+                u = uvp.tile([P, 512], F32, name="u", tag="u")
+                hold["u"] = u
+                nc.vector.tensor_tensor(
+                    out=u.rearrange("p (g j) -> p g j", j=64),
+                    in0=t.rearrange("p (g j) -> p g j", j=64),
+                    in1=cos_t[:, st, :].unsqueeze(1).to_broadcast([P, 8, 64]),
+                    op=ALU.mult,
+                )
+
+            def unit_v():
+                v = uvp.tile([P, 512], F32, name="v", tag="v")
+                hold["v"] = v
+                v4 = v.rearrange("p (h e j) -> p h e j", e=2, j=64)
+                t4 = t.rearrange("p (h e j) -> p h e j", e=2, j=64)
+                nc.vector.tensor_tensor(
+                    out=v4[:, :, 0, :], in0=t4[:, :, 1, :],
+                    in1=nsin_t[:, st, :].unsqueeze(1).to_broadcast([P, 4, 64]), op=ALU.mult,
+                )
+                nc.vector.tensor_tensor(
+                    out=v4[:, :, 1, :], in0=t4[:, :, 0, :],
+                    in1=sin_t[:, st, :].unsqueeze(1).to_broadcast([P, 4, 64]), op=ALU.mult,
+                )
+
+            def unit_r():
+                o3 = otiles[tt].rearrange("p (h c) -> p h c", c=HEAD_OUT)
+                hs = slice(4 * quad, 4 * quad + 4)
+                nc.vector.tensor_tensor(
+                    out=o3[:, hs, 1 + NOPE : HEAD_OUT].rearrange("p h (j e) -> p h j e", e=2),
+                    in0=hold["u"].rearrange("p (h e j) -> p h j e", e=2, j=64),
+                    in1=hold["v"].rearrange("p (h e j) -> p h j e", e=2, j=64),
+                    op=ALU.add,
+                )
+                for h in range(4 * quad, 4 * quad + 4):
+                    squares.append((o3[:, h, 1 + NOPE : HEAD_OUT], ssq_pe[:, tt, h : h + 1], ROPE))
+                half = quad // 2
+                i0 = 4 * (quad % 2)
+                base = HALF_COLS * half
+                rows = slice(P * tt, P * (tt + 1))
+                sb = otiles[tt][:, base : base + 1536].rearrange("p (i w) -> p i w", w=192)
+                hb = out_rows[rows, base : base + 1536].rearrange("p (i w) -> p i w", w=192)
+                nc.sync.dma_start(out=hb[:, i0 : i0 + 4, 72:192], in_=sb[:, i0 : i0 + 4, 72:192])
+                if i0 == 4:
+                    nc.sync.dma_start(
+                        out=out_rows[rows, base + 1536 : base + HALF_COLS],
+                        in_=otiles[tt][:, base + 1536 : base + HALF_COLS],
+                    )
+                r_done[(tt, half)] = r_done.get((tt, half), 0) + 1
+                try_finalize(tt, half)
+
+            return [unit_u, unit_v, unit_r]
+
+        def emit_units(n):
+            for unused in range(n):
+                if unit_pos[0] < len(units):
+                    units[unit_pos[0]]()
+                    unit_pos[0] += 1
+
+        nc.vector.memset(zrhs.bitcast(I32), 0)
+        nc.vector.memset(ones_bf[:, :], 1.0)
+        nc.vector.memset(brow.bitcast(I32), 0)
+        nc.vector.memset(one_col[:, :], 1.0)
+        make_identity(nc, ident[:, :])
+        nc.scalar.dma_start(out=brow[0:1, :], in_=wq_b.rearrange("(o n) -> o n", o=1))
+        nc.scalar.dma_start(out=cos_t[:, :, :], in_=freqs_cos.rearrange("(t p) j -> p t j", p=P))
+        nc.scalar.dma_start(out=sin_t[:, :, :], in_=freqs_sin.rearrange("(t p) j -> p t j", p=P))
+        nc.scalar.activation(out=scr_col[:, :], in_=one_col[:, :], func=ACT.Sqrt)
+        for i in range(RAW_BUFS):
+            emit_load(i)
+        emit_dummies(WARMUP)
+        nc.vector.tensor_copy(
+            out=perm.rearrange("p (e j) -> p e j", e=2), in_=ident.rearrange("p (j e) -> p e j", e=2)
+        )
+        nc.vector.tensor_scalar_mul(out=nsin_t[:, :, :], in0=sin_t[:, :, :], scalar1=-1.0)
+
+        for i in range(HEAD_RUNS):
+            emit_run(i)
+            if i + RAW_BUFS < N_RUNS:
+                emit_load(i + RAW_BUFS)
+            if i < 3:
+                emit_bias(2 * i)
+                emit_bias(2 * i + 1)
+            else:
+                emit_dummies(2)
+            emit_quant(i)
+
+        for c in range(len(CHUNKS)):
+            kind, idx = CHUNKS[c]
+            for hf in range(2):
+                i = HEAD_RUNS + 2 * c + hf
+                if i < N_RUNS:
+                    emit_run(i)
+                    if i + RAW_BUFS < N_RUNS:
+                        emit_load(i + RAW_BUFS)
+                flush_squares()
+                if i < N_RUNS:
+                    emit_quant(i)
+                fresh = []
+                for t2 in range(2):
+                    tt = 2 * hf + t2
+                    acc = emit_mx(c, tt)
+                    if kind == "P":
+                        t = evac_pe(acc, idx, tt)
+                        fresh.append(rope_units(t, idx, tt))
+                    else:
+                        evac_nope(acc, idx, tt)
+                    emit_units(UNITS_PER_BANK)
+                if fresh:
+                    for step in range(3):
+                        units.append(fresh[0][step])
+                        units.append(fresh[1][step])
+        emit_units(len(units))
+        flush_squares()

@@ -31,7 +31,8 @@ N_RUNS = 2 + 2 * len(CHUNKS)
 RAW_BUFS = 6
 HEAD_RUNS = 4
 WARMUP = 6
-UNITS_PER_BANK = 2
+W_ON_GPSIMD = True
+R_AFTER = {"P": (1, 0), "N": (2, 1)}
 
 
 def tile_lorentzmla_pb_kernel(tc, x, freqs_cos, freqs_sin, wq_w, wq_b, out):
@@ -46,8 +47,8 @@ def tile_lorentzmla_pb_kernel(tc, x, freqs_cos, freqs_sin, wq_w, wq_b, out):
         rawp = ctx.enter_context(tc.tile_pool(name="rawp", bufs=RAW_BUFS))
         grpp = ctx.enter_context(tc.tile_pool(name="grpp", bufs=3))
         codep = ctx.enter_context(tc.tile_pool(name="codep", bufs=3))
-        tpool = ctx.enter_context(tc.tile_pool(name="tpool", bufs=8))
-        uvp = ctx.enter_context(tc.tile_pool(name="uvp", bufs=4))
+        mpool = ctx.enter_context(tc.tile_pool(name="mpool", bufs=3))
+        wpool = ctx.enter_context(tc.tile_pool(name="wpool", bufs=8))
         junkp = ctx.enter_context(tc.tile_pool(name="junkp", bufs=2))
         ps_tr = ctx.enter_context(tc.psum_pool(name="ps_tr", bufs=4))
         ps_mx = ctx.enter_context(tc.psum_pool(name="ps_mx", bufs=4))
@@ -55,13 +56,18 @@ def tile_lorentzmla_pb_kernel(tc, x, freqs_cos, freqs_sin, wq_w, wq_b, out):
 
         ident = const.tile([P, P], F32, name="ident")
         perm = const.tile([P, P], F32, name="perm")
-        ones_bf = const.tile([P, P], BF16, name="ones_bf")
+        ident_b = const.tile([P, P], BF16, name="ident_b")
+        eye2 = const.tile([P, 64], BF16, name="eye2")
         zrhs = const.tile([P, 512], BF16, name="zrhs")
-        brow = const.tile([P, HEADS * QK], BF16, name="brow")
-        b_bc = const.tile([P, HEADS * QK], F32, name="b_bc")
-        cos_t = const.tile([P, 2, 64], BF16, name="cos_t")
-        sin_t = const.tile([P, 2, 64], BF16, name="sin_t")
-        nsin_t = const.tile([P, 2, 64], BF16, name="nsin_t")
+        cs = const.tile([P, 2, 2, 64], BF16, name="cs")
+        nsin = const.tile([P, 2, 64], BF16, name="nsin")
+        cs_t = const.tile([P, 2, P], BF16, name="cs_t")
+        bt = const.tile([P, P], BF16, name="bt")
+        bt2 = const.tile([P, 2, P], BF16, name="bt2")
+        coef = const.tile([P, HEADS, 2], BF16, name="coef")
+        dmat = const.tile([P, HEADS * ROPE], BF16, name="dmat")
+        rb = const.tile([P, 2, HEADS * ROPE], F32, name="rb")
+        b_bc = const.tile([P, HEADS * QK], BF16, name="b_bc")
         one_col = const.tile([P, 1], F32, name="one_col")
         scr_col = const.tile([P, 1], F32, name="scr_col")
         xq = const.tile([P, 2, 1024], U32, name="xq", align_bytes=64)
@@ -78,20 +84,23 @@ def tile_lorentzmla_pb_kernel(tc, x, freqs_cos, freqs_sin, wq_w, wq_b, out):
         groups = {}
         wcodes = {}
         wscales = {}
-        units = []
-        unit_pos = [0]
+        r_units = []
+        r_pos = [0]
         squares = []
-        r_done = {}
-        nope_done = {}
+        sq_count = {}
+        finals = []
 
         def emit_load(i):
             raw = rawp.tile([P, 4096], BF16, name="raw", tag="raw")
             raws[i] = raw
             if i < 2:
-                nc.sync.dma_start(
-                    out=raw.rearrange("p (t k) -> p t k", t=2),
-                    in_=x_rows[256 * i : 256 * (i + 1), :].rearrange("(t p) k -> p t k", p=P),
-                )
+                dst = raw.rearrange("p (t k) -> p t k", t=2)
+                src = x_rows[256 * i : 256 * (i + 1), :].rearrange("(t p) k -> p t k", p=P)
+                if i == 0:
+                    nc.sync.dma_start(out=dst[:, :, 0:1024], in_=src[:, :, 0:1024])
+                    nc.sync.dma_start(out=dst[:, :, 1024:2048], in_=src[:, :, 1024:2048])
+                else:
+                    nc.sync.dma_start(out=dst, in_=src)
                 return
             kind, idx = CHUNKS[(i - 2) // 2]
             hf = (i - 2) % 2
@@ -129,12 +138,9 @@ def tile_lorentzmla_pb_kernel(tc, x, freqs_cos, freqs_sin, wq_w, wq_b, out):
                             mat[:, :],
                         )
             for k in range(4):
-                dst = grp_words[:, 256 * k : 256 * (k + 1), :]
-                src = banks[k].rearrange("p u c -> p c u")
-                if i < HEAD_RUNS and k % 2 == 1:
-                    nc.vector.tensor_copy(out=dst, in_=src)
-                else:
-                    nc.scalar.copy(out=dst, in_=src)
+                nc.scalar.copy(
+                    out=grp_words[:, 256 * k : 256 * (k + 1), :], in_=banks[k].rearrange("p u c -> p c u")
+                )
 
         def emit_quant(i):
             flat = groups[i].rearrange("p c t -> p (c t)")
@@ -156,13 +162,13 @@ def tile_lorentzmla_pb_kernel(tc, x, freqs_cos, freqs_sin, wq_w, wq_b, out):
         def emit_dummies(n):
             bank = ps_mx.tile([P, 512], F32, name="acc", tag="acc")
             for unused in range(n):
-                nc.tensor.matmul(bank[:, :], lhsT=ones_bf[:, :], rhs=zrhs[:, :], start=True, stop=True)
+                nc.tensor.matmul(bank[:, :], lhsT=ident_b[:, :], rhs=zrhs[:, :], start=True, stop=True)
 
-        def emit_bias(k):
+        def emit_rb(st, quad):
             bank = ps_mx.tile([P, 512], F32, name="acc", tag="acc")
-            cols = slice(512 * k, 512 * (k + 1))
-            nc.tensor.matmul(bank[:, :], lhsT=ones_bf[:, :], rhs=brow[:, cols], start=True, stop=True)
-            nc.vector.tensor_copy(out=b_bc[:, cols], in_=bank[:, :])
+            cols = slice(512 * quad, 512 * (quad + 1))
+            nc.tensor.matmul(bank[:, :], lhsT=cs_t[:, st, :], rhs=dmat[:, cols], start=True, stop=True)
+            nc.vector.tensor_copy(out=rb[:, st, cols], in_=bank[:, :])
 
         def emit_mx(c, tt):
             acc = ps_mx.tile([P, 512], F32, name="acc", tag="acc")
@@ -181,29 +187,29 @@ def tile_lorentzmla_pb_kernel(tc, x, freqs_cos, freqs_sin, wq_w, wq_b, out):
                 )
             return acc
 
-        def flush_squares():
-            for (src, dst, width) in squares:
+        def flush_scalar():
+            for (tt, half) in finals:
+                hs = slice(8 * half, 8 * half + 8)
+                o3 = otiles[tt].rearrange("p (h c) -> p h c", c=HEAD_OUT)
+                nc.scalar.activation(
+                    out=o3[:, hs, 0:1], in_=tot[:, tt, hs].unsqueeze(2), func=ACT.Sqrt, bias=one_col[:, 0:1]
+                )
+                base = HALF_COLS * half
+                sb = otiles[tt][:, base : base + 1536].rearrange("p (i w) -> p i w", w=192)
+                hb = out_rows[P * tt : P * (tt + 1), base : base + 1536].rearrange("p (i w) -> p i w", w=192)
+                nc.sync.dma_start(out=hb[:, :, 0:72], in_=sb[:, :, 0:72])
+            finals.clear()
+            for (src, dst, width, tt, half) in squares:
                 junk = junkp.tile([P, ROPE], F32, name="junk", tag="junk")
                 nc.scalar.activation(out=junk[:, 0:width], in_=src, func=ACT.Square, accum_out=dst)
+                sq_count[(tt, half)] = sq_count.get((tt, half), 0) + 1
+                if sq_count[(tt, half)] == 16:
+                    hs = slice(8 * half, 8 * half + 8)
+                    nc.gpsimd.tensor_tensor(
+                        out=tot[:, tt, hs], in0=ssq_pe[:, tt, hs], in1=ssq_np[:, tt, hs], op=ALU.add
+                    )
+                    finals.append((tt, half))
             squares.clear()
-
-        def try_finalize(tt, half):
-            if not nope_done.get((tt, half), False):
-                return
-            if r_done.get((tt, half), 0) < 2:
-                return
-            flush_squares()
-            hs = slice(8 * half, 8 * half + 8)
-            nc.vector.scalar_tensor_tensor(
-                out=tot[:, tt, hs], in0=ssq_pe[:, tt, hs], scalar=1.0, in1=ssq_np[:, tt, hs],
-                op0=ALU.add, op1=ALU.add,
-            )
-            o3 = otiles[tt].rearrange("p (h c) -> p h c", c=HEAD_OUT)
-            nc.scalar.activation(out=o3[:, hs, 0:1], in_=tot[:, tt, hs].unsqueeze(2), func=ACT.Sqrt)
-            base = HALF_COLS * half
-            sb = otiles[tt][:, base : base + 1536].rearrange("p (i w) -> p i w", w=192)
-            hb = out_rows[P * tt : P * (tt + 1), base : base + 1536].rearrange("p (i w) -> p i w", w=192)
-            nc.sync.dma_start(out=hb[:, :, 0:72], in_=sb[:, :, 0:72])
 
         def evac_nope(acc, half, tt):
             hs = slice(8 * half, 8 * half + 8)
@@ -216,61 +222,44 @@ def tile_lorentzmla_pb_kernel(tc, x, freqs_cos, freqs_sin, wq_w, wq_b, out):
                 op=ALU.add,
             )
             for h in range(8 * half, 8 * half + 8):
-                squares.append((o3[:, h, 1 : 1 + NOPE], ssq_np[:, tt, h : h + 1], NOPE))
-            nope_done[(tt, half)] = True
-            try_finalize(tt, half)
+                squares.append((o3[:, h, 1 : 1 + NOPE], ssq_np[:, tt, h : h + 1], NOPE, tt, half))
 
         def evac_pe(acc, quad, tt):
-            t = tpool.tile([P, 512], F32, name="t", tag="t")
-            b3 = b_bc.rearrange("p (h r) -> p h r", r=QK)
-            nc.vector.tensor_tensor(
-                out=t.rearrange("p (h e j) -> p h e j", e=2, j=64),
-                in0=acc.rearrange("p (h e j) -> p h e j", e=2, j=64),
-                in1=b3[:, 4 * quad : 4 * quad + 4, NOPE:QK].rearrange("p h (j e) -> p h e j", e=2),
-                op=ALU.add,
-            )
-            return t
-
-        def rope_units(t, quad, tt):
             st = tt % 2
-            hold = {}
-
-            def unit_u():
-                u = uvp.tile([P, 512], F32, name="u", tag="u")
-                hold["u"] = u
-                nc.vector.tensor_tensor(
-                    out=u.rearrange("p (g j) -> p g j", j=64),
-                    in0=t.rearrange("p (g j) -> p g j", j=64),
-                    in1=cos_t[:, st, :].unsqueeze(1).to_broadcast([P, 8, 64]),
-                    op=ALU.mult,
-                )
-
-            def unit_v():
-                v = uvp.tile([P, 512], F32, name="v", tag="v")
-                hold["v"] = v
-                v4 = v.rearrange("p (h e j) -> p h e j", e=2, j=64)
-                t4 = t.rearrange("p (h e j) -> p h e j", e=2, j=64)
-                nc.vector.tensor_tensor(
-                    out=v4[:, :, 0, :], in0=t4[:, :, 1, :],
-                    in1=nsin_t[:, st, :].unsqueeze(1).to_broadcast([P, 4, 64]), op=ALU.mult,
-                )
-                nc.vector.tensor_tensor(
-                    out=v4[:, :, 1, :], in0=t4[:, :, 0, :],
-                    in1=sin_t[:, st, :].unsqueeze(1).to_broadcast([P, 4, 64]), op=ALU.mult,
-                )
+            m1 = mpool.tile([P, 512], F32, name="m1", tag="m1")
+            m2 = mpool.tile([P, 512], F32, name="m2", tag="m2")
+            a4 = acc.rearrange("p (h e j) -> p h e j", e=2, j=64)
+            m24 = m2.rearrange("p (h e j) -> p h e j", e=2, j=64)
+            nc.vector.tensor_tensor(
+                out=m1.rearrange("p (g j) -> p g j", j=64),
+                in0=acc.rearrange("p (g j) -> p g j", j=64),
+                in1=cs[:, st, 0, :].unsqueeze(1).to_broadcast([P, 8, 64]),
+                op=ALU.mult,
+            )
+            nc.vector.tensor_tensor(
+                out=m24[:, :, 0, :], in0=a4[:, :, 1, :],
+                in1=nsin[:, st, :].unsqueeze(1).to_broadcast([P, 4, 64]), op=ALU.mult,
+            )
+            nc.vector.tensor_tensor(
+                out=m24[:, :, 1, :], in0=a4[:, :, 0, :],
+                in1=cs[:, st, 1, :].unsqueeze(1).to_broadcast([P, 4, 64]), op=ALU.mult,
+            )
+            w = wpool.tile([P, 512], F32, name="w", tag="w")
+            add_engine = nc.gpsimd if W_ON_GPSIMD else nc.vector
+            add_engine.tensor_tensor(out=w[:, :], in0=m1[:, :], in1=m2[:, :], op=ALU.add)
 
             def unit_r():
                 o3 = otiles[tt].rearrange("p (h c) -> p h c", c=HEAD_OUT)
                 hs = slice(4 * quad, 4 * quad + 4)
                 nc.vector.tensor_tensor(
                     out=o3[:, hs, 1 + NOPE : HEAD_OUT].rearrange("p h (j e) -> p h j e", e=2),
-                    in0=hold["u"].rearrange("p (h e j) -> p h j e", e=2, j=64),
-                    in1=hold["v"].rearrange("p (h e j) -> p h j e", e=2, j=64),
+                    in0=w.rearrange("p (h e j) -> p h j e", e=2, j=64),
+                    in1=rb[:, st, 512 * quad : 512 * (quad + 1)].rearrange("p (h e j) -> p h j e", e=2, j=64),
                     op=ALU.add,
                 )
-                for h in range(4 * quad, 4 * quad + 4):
-                    squares.append((o3[:, h, 1 + NOPE : HEAD_OUT], ssq_pe[:, tt, h : h + 1], ROPE))
                 half = quad // 2
+                for h in range(4 * quad, 4 * quad + 4):
+                    squares.append((o3[:, h, 1 + NOPE : HEAD_OUT], ssq_pe[:, tt, h : h + 1], ROPE, tt, half))
                 i0 = 4 * (quad % 2)
                 base = HALF_COLS * half
                 rows = slice(P * tt, P * (tt + 1))
@@ -282,41 +271,60 @@ def tile_lorentzmla_pb_kernel(tc, x, freqs_cos, freqs_sin, wq_w, wq_b, out):
                         out=out_rows[rows, base + 1536 : base + HALF_COLS],
                         in_=otiles[tt][:, base + 1536 : base + HALF_COLS],
                     )
-                r_done[(tt, half)] = r_done.get((tt, half), 0) + 1
-                try_finalize(tt, half)
 
-            return [unit_u, unit_v, unit_r]
+            r_units.append(unit_r)
 
-        def emit_units(n):
+        def emit_r(n):
             for unused in range(n):
-                if unit_pos[0] < len(units):
-                    units[unit_pos[0]]()
-                    unit_pos[0] += 1
+                if r_pos[0] < len(r_units):
+                    r_units[r_pos[0]]()
+                    r_pos[0] += 1
 
+        nc.vector.memset(bt.bitcast(I32), 0)
         nc.vector.memset(zrhs.bitcast(I32), 0)
-        nc.vector.memset(ones_bf[:, :], 1.0)
-        nc.vector.memset(brow.bitcast(I32), 0)
         nc.vector.memset(one_col[:, :], 1.0)
         make_identity(nc, ident[:, :])
-        nc.scalar.dma_start(out=brow[0:1, :], in_=wq_b.rearrange("(o n) -> o n", o=1))
-        nc.scalar.dma_start(out=cos_t[:, :, :], in_=freqs_cos.rearrange("(t p) j -> p t j", p=P))
-        nc.scalar.dma_start(out=sin_t[:, :, :], in_=freqs_sin.rearrange("(t p) j -> p t j", p=P))
+        nc.sync.dma_start(out=cs[:, :, 0, :], in_=freqs_cos.rearrange("(t p) j -> p t j", p=P))
+        nc.sync.dma_start(out=cs[:, :, 1, :], in_=freqs_sin.rearrange("(t p) j -> p t j", p=P))
+        nc.sync.dma_start(out=bt[0:HEADS, :], in_=wq_b.rearrange("(h r) -> h r", r=QK)[:, NOPE:QK])
         nc.scalar.activation(out=scr_col[:, :], in_=one_col[:, :], func=ACT.Sqrt)
         for i in range(RAW_BUFS):
             emit_load(i)
+        nc.sync.dma_start(out=b_bc[:, :], in_=wq_b.partition_broadcast(P))
+
+        nc.vector.tensor_copy(out=ident_b[:, :], in_=ident[:, :])
         emit_dummies(WARMUP)
         nc.vector.tensor_copy(
             out=perm.rearrange("p (e j) -> p e j", e=2), in_=ident.rearrange("p (j e) -> p e j", e=2)
         )
-        nc.vector.tensor_scalar_mul(out=nsin_t[:, :, :], in0=sin_t[:, :, :], scalar1=-1.0)
+        nc.vector.tensor_tensor(out=eye2[:, :], in0=ident[:, 0:64], in1=ident[:, 64:128], op=ALU.add)
+        nc.vector.tensor_scalar_mul(out=nsin[:, :, :], in0=cs[:, :, 1, :], scalar1=-1.0)
+        bt_je = bt.rearrange("p (j e) -> p e j", e=2)
+        nc.vector.tensor_copy(out=bt2[:, 0, 0:64], in_=bt_je[:, 0, :])
+        nc.vector.tensor_scalar_mul(out=bt2[:, 0, 64:128], in0=bt_je[:, 1, :], scalar1=-1.0)
+        nc.vector.tensor_copy(out=bt2[:, 1, 0:64], in_=bt_je[:, 1, :])
+        nc.vector.tensor_copy(out=bt2[:, 1, 64:128], in_=bt_je[:, 0, :])
+        small = ps_tr.tile([P, 4, P], BF16, name="trb", tag="trb")
+        for st in range(2):
+            nc.tensor.transpose(small[:, st, :], cs[:, st, :, :].rearrange("p a j -> p (a j)"), ident_b[:, :])
+        for e in range(2):
+            nc.tensor.transpose(small[:, 2 + e, :], bt2[:, e, :], ident_b[:, :])
+        nc.scalar.copy(out=cs_t[:, :, :], in_=small[:, 0:2, :])
+        nc.vector.tensor_copy(out=coef[:, :, :], in_=small[:, 2:4, 0:HEADS].rearrange("p e h -> p h e"))
+        nc.vector.tensor_tensor(
+            out=dmat.rearrange("p (g j) -> p g j", j=64),
+            in0=eye2[:, :].unsqueeze(1).to_broadcast([P, 2 * HEADS, 64]),
+            in1=coef.rearrange("p h e -> p (h e)").unsqueeze(2).to_broadcast([P, 2 * HEADS, 64]),
+            op=ALU.mult,
+        )
 
         for i in range(HEAD_RUNS):
             emit_run(i)
             if i + RAW_BUFS < N_RUNS:
                 emit_load(i + RAW_BUFS)
-            if i < 3:
-                emit_bias(2 * i)
-                emit_bias(2 * i + 1)
+            if i == 1 or i == 2:
+                for quad in range(4):
+                    emit_rb(i - 1, quad)
             else:
                 emit_dummies(2)
             emit_quant(i)
@@ -329,22 +337,19 @@ def tile_lorentzmla_pb_kernel(tc, x, freqs_cos, freqs_sin, wq_w, wq_b, out):
                     emit_run(i)
                     if i + RAW_BUFS < N_RUNS:
                         emit_load(i + RAW_BUFS)
-                flush_squares()
+                flush_scalar()
                 if i < N_RUNS:
                     emit_quant(i)
-                fresh = []
                 for t2 in range(2):
                     tt = 2 * hf + t2
                     acc = emit_mx(c, tt)
                     if kind == "P":
-                        t = evac_pe(acc, idx, tt)
-                        fresh.append(rope_units(t, idx, tt))
+                        evac_pe(acc, idx, tt)
                     else:
                         evac_nope(acc, idx, tt)
-                    emit_units(UNITS_PER_BANK)
-                if fresh:
-                    for step in range(3):
-                        units.append(fresh[0][step])
-                        units.append(fresh[1][step])
-        emit_units(len(units))
-        flush_squares()
+                    emit_r(R_AFTER[kind][t2])
+        while r_pos[0] < len(r_units):
+            emit_r(1)
+            flush_scalar()
+        flush_scalar()
+        flush_scalar()

@@ -26,13 +26,16 @@ HALF_COLS = 8 * HEAD_OUT
 
 FLOPS = 2 * TOKENS * HEADS * QK * DIM
 
-CHUNKS = (("P", 0), ("P", 1), ("N", 0), ("P", 2), ("P", 3), ("N", 1))
-N_RUNS = 2 + 2 * len(CHUNKS)
-RAW_BUFS = 6
+CHUNKS = (("P", 0), ("N", 0), ("P", 1), ("P", 2), ("N", 1), ("P", 3))
+RUNS = (("x", 0), ("w", 0, 0), ("w", 0, 1), ("x", 1)) + tuple(("w", c, hf) for c in range(1, 6) for hf in range(2))
+N_RUNS = len(RUNS)
+RAW_BUFS = 5
 HEAD_RUNS = 4
+RUNS_BEFORE_STEP = {0: (), 1: (4,), 2: (5, 6)}
 WARMUP = 6
-W_ON_GPSIMD = True
-R_AFTER = {"P": (1, 0), "N": (2, 1)}
+V_EVAC = {"H": 1, "P": 0, "N": 0}
+UNITS_AFTER = {"P": (0, 1), "N": (1, 1)}
+QUADS_PER_FLUSH = 2
 
 
 def tile_lorentzmla_pb_kernel(tc, x, freqs_cos, freqs_sin, wq_w, wq_b, out):
@@ -41,14 +44,16 @@ def tile_lorentzmla_pb_kernel(tc, x, freqs_cos, freqs_sin, wq_w, wq_b, out):
     out_rows = out.rearrange("b s h c -> (b s) (h c)")
     w_pe = wq_w.rearrange("(h r) k -> r h k", r=QK)
     w_np = wq_w.rearrange("(q a r) k -> a r q k", a=2, r=QK)
+    b_hr = wq_b.rearrange("(o h r) -> o h r", o=1, r=QK)
+    cos_src = freqs_cos.rearrange("(t p) j -> p t j", p=P)
+    sin_src = freqs_sin.rearrange("(t p) j -> p t j", p=P)
 
     with ExitStack() as ctx:
         const = ctx.enter_context(tc.tile_pool(name="const", bufs=1))
         rawp = ctx.enter_context(tc.tile_pool(name="rawp", bufs=RAW_BUFS))
         grpp = ctx.enter_context(tc.tile_pool(name="grpp", bufs=3))
         codep = ctx.enter_context(tc.tile_pool(name="codep", bufs=3))
-        mpool = ctx.enter_context(tc.tile_pool(name="mpool", bufs=3))
-        wpool = ctx.enter_context(tc.tile_pool(name="wpool", bufs=8))
+        mpool = ctx.enter_context(tc.tile_pool(name="mpool", bufs=5))
         junkp = ctx.enter_context(tc.tile_pool(name="junkp", bufs=2))
         ps_tr = ctx.enter_context(tc.psum_pool(name="ps_tr", bufs=4))
         ps_mx = ctx.enter_context(tc.psum_pool(name="ps_mx", bufs=4))
@@ -57,28 +62,27 @@ def tile_lorentzmla_pb_kernel(tc, x, freqs_cos, freqs_sin, wq_w, wq_b, out):
         ident = const.tile([P, P], F32, name="ident")
         perm = const.tile([P, P], F32, name="perm")
         ident_b = const.tile([P, P], BF16, name="ident_b")
+        ones_b = const.tile([P, P], BF16, name="ones_b")
         eye2 = const.tile([P, 64], BF16, name="eye2")
         zrhs = const.tile([P, 512], BF16, name="zrhs")
         cs = const.tile([P, 2, 2, 64], BF16, name="cs")
-        nsin = const.tile([P, 2, 64], BF16, name="nsin")
+        tab1 = const.tile([P, 2, 2, 64, 2], BF16, name="tab1")
+        tabf = const.tile([P, 2, 4, 256], BF16, name="tabf")
         cs_t = const.tile([P, 2, P], BF16, name="cs_t")
         bt = const.tile([P, P], BF16, name="bt")
         bt2 = const.tile([P, 2, P], BF16, name="bt2")
         coef = const.tile([P, HEADS, 2], BF16, name="coef")
         dmat = const.tile([P, HEADS * ROPE], BF16, name="dmat")
         rb = const.tile([P, 2, HEADS * ROPE], F32, name="rb")
-        b_bc = const.tile([P, HEADS * QK], BF16, name="b_bc")
+        brow = const.tile([P, HEADS * NOPE], BF16, name="brow")
+        b_np = const.tile([P, HEADS * NOPE], F32, name="b_np")
         one_col = const.tile([P, 1], F32, name="one_col")
         scr_col = const.tile([P, 1], F32, name="scr_col")
         xq = const.tile([P, 2, 1024], U32, name="xq", align_bytes=64)
         xs = const.tile([P, 2, 1024], U8, name="xs", align_bytes=64)
-        ssq_pe = const.tile([P, 4, HEADS], F32, name="ssq_pe")
-        ssq_np = const.tile([P, 4, HEADS], F32, name="ssq_np")
         tot = const.tile([P, 4, HEADS], F32, name="tot")
-        otiles = []
-        for tt in range(4):
-            o_tile = const.tile([P, OUT_COLS], F32, name="o_tile%d" % tt)
-            otiles.append(o_tile)
+        o_all = const.tile([P, 4, OUT_COLS], F32, name="o_all")
+        o4 = o_all.rearrange("p t (h c) -> p t h c", c=HEAD_OUT)
 
         raws = {}
         groups = {}
@@ -86,25 +90,25 @@ def tile_lorentzmla_pb_kernel(tc, x, freqs_cos, freqs_sin, wq_w, wq_b, out):
         wscales = {}
         r_units = []
         r_pos = [0]
-        squares = []
-        sq_count = {}
-        finals = []
+        written = {}
+        ripe = []
+        fresh = []
 
         def emit_load(i):
             raw = rawp.tile([P, 4096], BF16, name="raw", tag="raw")
             raws[i] = raw
-            if i < 2:
+            run = RUNS[i]
+            if run[0] == "x":
                 dst = raw.rearrange("p (t k) -> p t k", t=2)
-                src = x_rows[256 * i : 256 * (i + 1), :].rearrange("(t p) k -> p t k", p=P)
+                src = x_rows[256 * run[1] : 256 * (run[1] + 1), :].rearrange("(t p) k -> p t k", p=P)
                 if i == 0:
                     nc.sync.dma_start(out=dst[:, :, 0:1024], in_=src[:, :, 0:1024])
                     nc.sync.dma_start(out=dst[:, :, 1024:2048], in_=src[:, :, 1024:2048])
                 else:
                     nc.sync.dma_start(out=dst, in_=src)
                 return
-            kind, idx = CHUNKS[(i - 2) // 2]
-            hf = (i - 2) % 2
-            cols = slice(1024 * hf, 1024 * (hf + 1))
+            kind, idx = CHUNKS[run[1]]
+            cols = slice(1024 * run[2], 1024 * (run[2] + 1))
             dst = raw.rearrange("p (q k) -> p q k", q=4)
             if kind == "P":
                 nc.sync.dma_start(out=dst, in_=w_pe[NOPE:QK, 4 * idx : 4 * idx + 4, cols])
@@ -115,20 +119,20 @@ def tile_lorentzmla_pb_kernel(tc, x, freqs_cos, freqs_sin, wq_w, wq_b, out):
                         in_=w_np[a, 0:NOPE, 4 * idx : 4 * idx + 4, cols],
                     )
 
-        def emit_run(i):
+        def emit_run(i, on_vector):
+            run = RUNS[i]
             words = raws[i].bitcast(F32)
             grp = grpp.tile([P, 1024, 4], BF16, name="grp", tag="grp", align_bytes=64)
             groups[i] = grp
             grp_words = grp.bitcast(F32)
-            is_pe = i >= 2 and CHUNKS[(i - 2) // 2][0] == "P"
-            mat = perm if is_pe else ident
+            mat = perm if (run[0] == "w" and CHUNKS[run[1]][0] == "P") else ident
             banks = []
             for k in range(4):
                 bank = ps_tr.tile([P, 2, 256], F32, name="trb", tag="trb")
                 banks.append(bank)
                 for u in range(2):
                     for r2 in range(2):
-                        if i < 2:
+                        if run[0] == "x":
                             start = 1024 * r2 + 256 * k + u
                         else:
                             start = 512 * (2 * (k % 2) + r2) + 256 * (k // 2) + u
@@ -138,23 +142,28 @@ def tile_lorentzmla_pb_kernel(tc, x, freqs_cos, freqs_sin, wq_w, wq_b, out):
                             mat[:, :],
                         )
             for k in range(4):
-                nc.scalar.copy(
-                    out=grp_words[:, 256 * k : 256 * (k + 1), :], in_=banks[k].rearrange("p u c -> p c u")
-                )
+                dst = grp_words[:, 256 * k : 256 * (k + 1), :]
+                src = banks[k].rearrange("p u c -> p c u")
+                if k >= 4 - on_vector:
+                    nc.vector.tensor_copy(out=dst, in_=src)
+                else:
+                    nc.scalar.copy(out=dst, in_=src)
+            if i + RAW_BUFS < N_RUNS:
+                emit_load(i + RAW_BUFS)
 
         def emit_quant(i):
+            run = RUNS[i]
             flat = groups[i].rearrange("p c t -> p (c t)")
-            if i < 2:
-                nc.vector.quantize_mx(out=xq[:, i, :].bitcast(E5M2X4), scales=xs[:, i, :], in_=flat)
+            if run[0] == "x":
+                nc.vector.quantize_mx(out=xq[:, run[1], :].bitcast(E5M2X4), scales=xs[:, run[1], :], in_=flat)
                 return
-            c = (i - 2) // 2
-            hf = (i - 2) % 2
-            if hf == 0:
+            c = run[1]
+            if run[2] == 0:
                 wq = codep.tile([P, 2048], U32, name="wq", tag="wq", align_bytes=64)
                 ws = codep.tile([P, 2048], U8, name="ws", tag="ws", align_bytes=64)
                 wcodes[c] = wq
                 wscales[c] = ws
-            cols = slice(1024 * hf, 1024 * (hf + 1))
+            cols = slice(1024 * run[2], 1024 * (run[2] + 1))
             nc.vector.quantize_mx(
                 out=wcodes[c][:, cols].bitcast(E4M3X4), scales=wscales[c][:, cols], in_=flat
             )
@@ -164,11 +173,19 @@ def tile_lorentzmla_pb_kernel(tc, x, freqs_cos, freqs_sin, wq_w, wq_b, out):
             for unused in range(n):
                 nc.tensor.matmul(bank[:, :], lhsT=ident_b[:, :], rhs=zrhs[:, :], start=True, stop=True)
 
-        def emit_rb(st, quad):
-            bank = ps_mx.tile([P, 512], F32, name="acc", tag="acc")
-            cols = slice(512 * quad, 512 * (quad + 1))
-            nc.tensor.matmul(bank[:, :], lhsT=cs_t[:, st, :], rhs=dmat[:, cols], start=True, stop=True)
-            nc.vector.tensor_copy(out=rb[:, st, cols], in_=bank[:, :])
+        def emit_bias_np():
+            for k in range(2):
+                bank = ps_mx.tile([P, 512], F32, name="acc", tag="acc")
+                cols = slice(512 * k, 512 * (k + 1))
+                nc.tensor.matmul(bank[:, :], lhsT=ones_b[:, :], rhs=brow[:, cols], start=True, stop=True)
+                nc.scalar.copy(out=b_np[:, cols], in_=bank[:, :])
+
+        def emit_rb(quad):
+            for st in range(2):
+                bank = ps_mx.tile([P, 512], F32, name="acc", tag="acc")
+                cols = slice(512 * quad, 512 * (quad + 1))
+                nc.tensor.matmul(bank[:, :], lhsT=cs_t[:, st, :], rhs=dmat[:, cols], start=True, stop=True)
+                nc.scalar.copy(out=rb[:, st, cols], in_=bank[:, :])
 
         def emit_mx(c, tt):
             acc = ps_mx.tile([P, 512], F32, name="acc", tag="acc")
@@ -187,92 +204,72 @@ def tile_lorentzmla_pb_kernel(tc, x, freqs_cos, freqs_sin, wq_w, wq_b, out):
                 )
             return acc
 
-        def flush_scalar():
-            for (tt, half) in finals:
-                hs = slice(8 * half, 8 * half + 8)
-                o3 = otiles[tt].rearrange("p (h c) -> p h c", c=HEAD_OUT)
+        def finish_quad(tt, quad):
+            hs = slice(4 * quad, 4 * quad + 4)
+            for h in range(4 * quad, 4 * quad + 4):
+                junk = junkp.tile([P, QK], F32, name="junk", tag="junk")
                 nc.scalar.activation(
-                    out=o3[:, hs, 0:1], in_=tot[:, tt, hs].unsqueeze(2), func=ACT.Sqrt, bias=one_col[:, 0:1]
+                    out=junk[:, :], in_=o4[:, tt, h, 1:HEAD_OUT], func=ACT.Square, accum_out=tot[:, tt, h : h + 1]
                 )
-                base = HALF_COLS * half
-                sb = otiles[tt][:, base : base + 1536].rearrange("p (i w) -> p i w", w=192)
-                hb = out_rows[P * tt : P * (tt + 1), base : base + 1536].rearrange("p (i w) -> p i w", w=192)
-                nc.sync.dma_start(out=hb[:, :, 0:72], in_=sb[:, :, 0:72])
-            finals.clear()
-            for (src, dst, width, tt, half) in squares:
-                junk = junkp.tile([P, ROPE], F32, name="junk", tag="junk")
-                nc.scalar.activation(out=junk[:, 0:width], in_=src, func=ACT.Square, accum_out=dst)
-                sq_count[(tt, half)] = sq_count.get((tt, half), 0) + 1
-                if sq_count[(tt, half)] == 16:
-                    hs = slice(8 * half, 8 * half + 8)
-                    nc.gpsimd.tensor_tensor(
-                        out=tot[:, tt, hs], in0=ssq_pe[:, tt, hs], in1=ssq_np[:, tt, hs], op=ALU.add
-                    )
-                    finals.append((tt, half))
-            squares.clear()
+            nc.scalar.activation(
+                out=o4[:, tt, hs, 0:1], in_=tot[:, tt, hs].unsqueeze(2), func=ACT.Sqrt, bias=one_col[:, 0:1]
+            )
+            base = HALF_COLS * (quad // 2)
+            lo = base + 768 * (quad % 2)
+            hi = base + (768 if quad % 2 == 0 else HALF_COLS)
+            nc.sync.dma_start(out=out_rows[P * tt : P * (tt + 1), lo:hi], in_=o_all[:, tt, lo:hi])
+
+        def mark(tt, quad):
+            written[(tt, quad)] = written.get((tt, quad), 0) + 1
+            if written[(tt, quad)] == 2:
+                fresh.append((tt, quad))
+
+        def flush_scalar(n):
+            for unused in range(n):
+                if ripe:
+                    tt, quad = ripe.pop(0)
+                    finish_quad(tt, quad)
+            ripe.extend(fresh)
+            fresh.clear()
 
         def evac_nope(acc, half, tt):
             hs = slice(8 * half, 8 * half + 8)
-            o3 = otiles[tt].rearrange("p (h c) -> p h c", c=HEAD_OUT)
-            b3 = b_bc.rearrange("p (h r) -> p h r", r=QK)
             nc.vector.tensor_tensor(
-                out=o3[:, hs, 1 : 1 + NOPE],
+                out=o4[:, tt, hs, 1 : 1 + NOPE],
                 in0=acc.rearrange("p (h n) -> p h n", n=NOPE),
-                in1=b3[:, hs, 0:NOPE],
+                in1=b_np[:, 512 * half : 512 * (half + 1)].rearrange("p (h n) -> p h n", n=NOPE),
                 op=ALU.add,
             )
-            for h in range(8 * half, 8 * half + 8):
-                squares.append((o3[:, h, 1 : 1 + NOPE], ssq_np[:, tt, h : h + 1], NOPE, tt, half))
+            mark(tt, 2 * half)
+            mark(tt, 2 * half + 1)
 
-        def evac_pe(acc, quad, tt):
+        def products(acc, tt, mpair):
             st = tt % 2
-            m1 = mpool.tile([P, 512], F32, name="m1", tag="m1")
-            m2 = mpool.tile([P, 512], F32, name="m2", tag="m2")
-            a4 = acc.rearrange("p (h e j) -> p h e j", e=2, j=64)
-            m24 = m2.rearrange("p (h e j) -> p h e j", e=2, j=64)
             nc.vector.tensor_tensor(
-                out=m1.rearrange("p (g j) -> p g j", j=64),
-                in0=acc.rearrange("p (g j) -> p g j", j=64),
-                in1=cs[:, st, 0, :].unsqueeze(1).to_broadcast([P, 8, 64]),
+                out=mpair[:, st, :].rearrange("p (g j e) -> p g j e", j=64, e=2),
+                in0=acc.rearrange("p (g j) -> p g j", j=64).unsqueeze(3).to_broadcast([P, 8, 64, 2]),
+                in1=tabf[:, st, :, :].rearrange("p h (a j e) -> p (h a) j e", j=64, e=2),
                 op=ALU.mult,
             )
-            nc.vector.tensor_tensor(
-                out=m24[:, :, 0, :], in0=a4[:, :, 1, :],
-                in1=nsin[:, st, :].unsqueeze(1).to_broadcast([P, 4, 64]), op=ALU.mult,
-            )
-            nc.vector.tensor_tensor(
-                out=m24[:, :, 1, :], in0=a4[:, :, 0, :],
-                in1=cs[:, st, 1, :].unsqueeze(1).to_broadcast([P, 4, 64]), op=ALU.mult,
-            )
-            w = wpool.tile([P, 512], F32, name="w", tag="w")
-            add_engine = nc.gpsimd if W_ON_GPSIMD else nc.vector
-            add_engine.tensor_tensor(out=w[:, :], in0=m1[:, :], in1=m2[:, :], op=ALU.add)
 
-            def unit_r():
-                o3 = otiles[tt].rearrange("p (h c) -> p h c", c=HEAD_OUT)
-                hs = slice(4 * quad, 4 * quad + 4)
-                nc.vector.tensor_tensor(
-                    out=o3[:, hs, 1 + NOPE : HEAD_OUT].rearrange("p h (j e) -> p h j e", e=2),
-                    in0=w.rearrange("p (h e j) -> p h j e", e=2, j=64),
-                    in1=rb[:, st, 512 * quad : 512 * (quad + 1)].rearrange("p (h e j) -> p h j e", e=2, j=64),
-                    op=ALU.add,
-                )
-                half = quad // 2
-                for h in range(4 * quad, 4 * quad + 4):
-                    squares.append((o3[:, h, 1 + NOPE : HEAD_OUT], ssq_pe[:, tt, h : h + 1], ROPE, tt, half))
-                i0 = 4 * (quad % 2)
-                base = HALF_COLS * half
-                rows = slice(P * tt, P * (tt + 1))
-                sb = otiles[tt][:, base : base + 1536].rearrange("p (i w) -> p i w", w=192)
-                hb = out_rows[rows, base : base + 1536].rearrange("p (i w) -> p i w", w=192)
-                nc.sync.dma_start(out=hb[:, i0 : i0 + 4, 72:192], in_=sb[:, i0 : i0 + 4, 72:192])
-                if i0 == 4:
-                    nc.sync.dma_start(
-                        out=out_rows[rows, base + 1536 : base + HALF_COLS],
-                        in_=otiles[tt][:, base + 1536 : base + HALF_COLS],
-                    )
+        def sum_products(mpair, lo, n):
+            mv = mpair.rearrange("p t (h a c) -> p a t h c", a=2, c=ROPE)
+            nc.vector.tensor_tensor(
+                out=mv[:, 0, lo : lo + n, :, :], in0=mv[:, 0, lo : lo + n, :, :], in1=mv[:, 1, lo : lo + n, :, :],
+                op=ALU.add,
+            )
 
-            r_units.append(unit_r)
+        def add_rb(mpair, quad, t0, lo, n):
+            hs = slice(4 * quad, 4 * quad + 4)
+            mv = mpair.rearrange("p t (h a c) -> p a t h c", a=2, c=ROPE)
+            nc.vector.tensor_tensor(
+                out=o4[:, t0 + lo : t0 + lo + n, hs, 1 + NOPE : HEAD_OUT],
+                in0=mv[:, 0, lo : lo + n, :, :],
+                in1=rb[:, lo : lo + n, 512 * quad : 512 * (quad + 1)].rearrange("p t (h c) -> p t h c", c=ROPE),
+                op=ALU.add,
+            )
+            for t in range(t0 + lo, t0 + lo + n):
+                mark(t, quad)
 
         def emit_r(n):
             for unused in range(n):
@@ -281,16 +278,19 @@ def tile_lorentzmla_pb_kernel(tc, x, freqs_cos, freqs_sin, wq_w, wq_b, out):
                     r_pos[0] += 1
 
         nc.vector.memset(bt.bitcast(I32), 0)
+        nc.vector.memset(brow.bitcast(I32), 0)
         nc.vector.memset(zrhs.bitcast(I32), 0)
+        nc.vector.memset(ones_b[:, :], 1.0)
         nc.vector.memset(one_col[:, :], 1.0)
         make_identity(nc, ident[:, :])
-        nc.sync.dma_start(out=cs[:, :, 0, :], in_=freqs_cos.rearrange("(t p) j -> p t j", p=P))
-        nc.sync.dma_start(out=cs[:, :, 1, :], in_=freqs_sin.rearrange("(t p) j -> p t j", p=P))
         nc.sync.dma_start(out=bt[0:HEADS, :], in_=wq_b.rearrange("(h r) -> h r", r=QK)[:, NOPE:QK])
+        nc.sync.dma_start(out=cs[:, :, 0, :], in_=cos_src)
+        nc.sync.dma_start(out=cs[:, :, 1, :], in_=sin_src)
+        emit_load(0)
+        nc.sync.dma_start(out=brow[0:1, :].rearrange("p (h n) -> p h n", n=NOPE), in_=b_hr[:, :, 0:NOPE])
         nc.scalar.activation(out=scr_col[:, :], in_=one_col[:, :], func=ACT.Sqrt)
-        for i in range(RAW_BUFS):
+        for i in range(1, RAW_BUFS):
             emit_load(i)
-        nc.sync.dma_start(out=b_bc[:, :], in_=wq_b.partition_broadcast(P))
 
         nc.vector.tensor_copy(out=ident_b[:, :], in_=ident[:, :])
         emit_dummies(WARMUP)
@@ -298,58 +298,88 @@ def tile_lorentzmla_pb_kernel(tc, x, freqs_cos, freqs_sin, wq_w, wq_b, out):
             out=perm.rearrange("p (e j) -> p e j", e=2), in_=ident.rearrange("p (j e) -> p e j", e=2)
         )
         nc.vector.tensor_tensor(out=eye2[:, :], in0=ident[:, 0:64], in1=ident[:, 64:128], op=ALU.add)
-        nc.vector.tensor_scalar_mul(out=nsin[:, :, :], in0=cs[:, :, 1, :], scalar1=-1.0)
-        bt_je = bt.rearrange("p (j e) -> p e j", e=2)
-        nc.vector.tensor_copy(out=bt2[:, 0, 0:64], in_=bt_je[:, 0, :])
-        nc.vector.tensor_scalar_mul(out=bt2[:, 0, 64:128], in0=bt_je[:, 1, :], scalar1=-1.0)
-        nc.vector.tensor_copy(out=bt2[:, 1, 0:64], in_=bt_je[:, 1, :])
-        nc.vector.tensor_copy(out=bt2[:, 1, 64:128], in_=bt_je[:, 0, :])
-        small = ps_tr.tile([P, 4, P], BF16, name="trb", tag="trb")
-        for st in range(2):
-            nc.tensor.transpose(small[:, st, :], cs[:, st, :, :].rearrange("p a j -> p (a j)"), ident_b[:, :])
-        for e in range(2):
-            nc.tensor.transpose(small[:, 2 + e, :], bt2[:, e, :], ident_b[:, :])
-        nc.scalar.copy(out=cs_t[:, :, :], in_=small[:, 0:2, :])
-        nc.vector.tensor_copy(out=coef[:, :, :], in_=small[:, 2:4, 0:HEADS].rearrange("p e h -> p h e"))
-        nc.vector.tensor_tensor(
-            out=dmat.rearrange("p (g j) -> p g j", j=64),
-            in0=eye2[:, :].unsqueeze(1).to_broadcast([P, 2 * HEADS, 64]),
-            in1=coef.rearrange("p h e -> p (h e)").unsqueeze(2).to_broadcast([P, 2 * HEADS, 64]),
-            op=ALU.mult,
-        )
 
-        for i in range(HEAD_RUNS):
-            emit_run(i)
-            if i + RAW_BUFS < N_RUNS:
-                emit_load(i + RAW_BUFS)
-            if i == 1 or i == 2:
-                for quad in range(4):
-                    emit_rb(i - 1, quad)
-            else:
-                emit_dummies(2)
-            emit_quant(i)
+        def emit_tables():
+            bt_je = bt.rearrange("p (j e) -> p e j", e=2)
+            nc.gpsimd.tensor_copy(out=bt2[:, 0, 0:64], in_=bt_je[:, 0, :])
+            nc.gpsimd.tensor_scalar(
+                out=bt2[:, 0, 64:128], in0=bt_je[:, 1, :], scalar1=-1.0, scalar2=0.0, op0=ALU.mult, op1=ALU.add
+            )
+            nc.gpsimd.tensor_copy(out=bt2[:, 1, 0:64], in_=bt_je[:, 1, :])
+            nc.gpsimd.tensor_copy(out=bt2[:, 1, 64:128], in_=bt_je[:, 0, :])
+            small = ps_tr.tile([P, 4, P], BF16, name="trb", tag="trb")
+            for st in range(2):
+                nc.tensor.transpose(small[:, st, :], cs[:, st, :, :].rearrange("p a j -> p (a j)"), ident_b[:, :])
+            for e in range(2):
+                nc.tensor.transpose(small[:, 2 + e, :], bt2[:, e, :], ident_b[:, :])
+            nc.scalar.copy(out=cs_t[:, :, :], in_=small[:, 0:2, :])
+            nc.scalar.copy(out=coef[:, :, :], in_=small[:, 2:4, 0:HEADS].rearrange("p e h -> p h e"))
+            nc.gpsimd.tensor_tensor(
+                out=dmat.rearrange("p (h j e) -> p h j e", j=64, e=2),
+                in0=eye2[:, :].unsqueeze(1).unsqueeze(3).to_broadcast([P, HEADS, 64, 2]),
+                in1=coef[:, :, :].unsqueeze(2).to_broadcast([P, HEADS, 64, 2]),
+                op=ALU.mult,
+            )
+            nc.vector.tensor_copy(out=tab1[:, :, 0, :, 0], in_=cs[:, :, 0, :])
+            nc.vector.tensor_copy(out=tab1[:, :, 0, :, 1], in_=cs[:, :, 1, :])
+            nc.vector.tensor_scalar_mul(out=tab1[:, :, 1, :, 0], in0=cs[:, :, 1, :], scalar1=-1.0)
+            nc.vector.tensor_copy(out=tab1[:, :, 1, :, 1], in_=cs[:, :, 0, :])
+            nc.vector.tensor_copy(
+                out=tabf[:, :, :, :],
+                in_=tab1.rearrange("p s a j e -> p s (a j e)").unsqueeze(2).to_broadcast([P, 2, 4, 256]),
+            )
 
-        for c in range(len(CHUNKS)):
+        emit_tables()
+        emit_run(0, V_EVAC["H"])
+        emit_dummies(2)
+        emit_quant(0)
+        emit_run(1, V_EVAC["H"])
+        emit_rb(0)
+        emit_quant(1)
+        emit_run(2, V_EVAC["H"])
+        emit_bias_np()
+        emit_quant(2)
+        emit_run(3, V_EVAC["H"])
+
+        n_steps = 2 * len(CHUNKS)
+        for step in range(n_steps):
+            c = step // 2
+            hf = step % 2
             kind, idx = CHUNKS[c]
-            for hf in range(2):
-                i = HEAD_RUNS + 2 * c + hf
-                if i < N_RUNS:
-                    emit_run(i)
-                    if i + RAW_BUFS < N_RUNS:
-                        emit_load(i + RAW_BUFS)
-                flush_scalar()
-                if i < N_RUNS:
-                    emit_quant(i)
-                for t2 in range(2):
-                    tt = 2 * hf + t2
-                    acc = emit_mx(c, tt)
-                    if kind == "P":
-                        evac_pe(acc, idx, tt)
-                    else:
-                        evac_nope(acc, idx, tt)
-                    emit_r(R_AFTER[kind][t2])
+            runs = RUNS_BEFORE_STEP.get(step, (step + 4,))
+            todo = [i for i in runs if i < N_RUNS]
+            for n, i in enumerate(todo):
+                if n > 0:
+                    emit_rb(1)
+                emit_run(i, V_EVAC[kind])
+            flush_scalar(QUADS_PER_FLUSH)
+            for i in todo:
+                emit_quant(i)
+            if kind == "P":
+                mpair = mpool.tile([P, 2, 1024], F32, name="mpair", tag="mpair")
+            for t2 in range(2):
+                tt = 2 * hf + t2
+                acc = emit_mx(c, tt)
+                if kind == "P":
+                    products(acc, tt, mpair)
+                    if step == n_steps - 1:
+                        r_units.append(lambda mp=mpair, s=t2: sum_products(mp, s, 1))
+                        r_units.append(lambda mp=mpair, q=idx, t=2 * hf, s=t2: add_rb(mp, q, t, s, 1))
+                else:
+                    evac_nope(acc, idx, tt)
+                emit_r(UNITS_AFTER[kind][t2])
+            if kind == "P" and step != n_steps - 1:
+                r_units.append(lambda mp=mpair: sum_products(mp, 0, 2))
+                r_units.append(lambda mp=mpair, q=idx, t=2 * hf: add_rb(mp, q, t, 0, 2))
+            if step == 0:
+                emit_quant(3)
+            if step == 3:
+                emit_rb(2)
+            if step == 4:
+                emit_rb(3)
         while r_pos[0] < len(r_units):
             emit_r(1)
-            flush_scalar()
-        flush_scalar()
-        flush_scalar()
+            flush_scalar(0)
+            flush_scalar(2)
+        flush_scalar(4)
+        flush_scalar(4)

@@ -26,7 +26,7 @@ HALF_COLS = 8 * HEAD_OUT
 
 FLOPS = 2 * TOKENS * HEADS * QK * DIM
 
-CHUNKS = (("P", 0), ("N", 0), ("P", 1), ("P", 2), ("N", 1), ("P", 3))
+CHUNKS = (("P", 0), ("P", 1), ("N", 0), ("P", 2), ("N", 1), ("P", 3))
 RUNS = (("x", 0), ("w", 0, 0), ("w", 0, 1), ("x", 1)) + tuple(("w", c, hf) for c in range(1, 6) for hf in range(2))
 N_RUNS = len(RUNS)
 RAW_BUFS = 5
@@ -362,15 +362,19 @@ def tile_lorentzmla_pb_kernel(tc, x, freqs_cos, freqs_sin, wq_w, wq_b, out):
                 acc = emit_mx(c, tt)
                 if kind == "P":
                     products(acc, tt, mpair)
-                    if step == n_steps - 1:
-                        r_units.append(lambda mp=mpair, s=t2: sum_products(mp, s, 1))
-                        r_units.append(lambda mp=mpair, q=idx, t=2 * hf, s=t2: add_rb(mp, q, t, s, 1))
                 else:
                     evac_nope(acc, idx, tt)
                 emit_r(UNITS_AFTER[kind][t2])
             if kind == "P" and step != n_steps - 1:
                 r_units.append(lambda mp=mpair: sum_products(mp, 0, 2))
                 r_units.append(lambda mp=mpair, q=idx, t=2 * hf: add_rb(mp, q, t, 0, 2))
+            if step == n_steps - 2:
+                emit_r(len(r_units))
+            if step == n_steps - 1:
+                for s in range(2):
+                    r_units.append(lambda mp=mpair, s=s: sum_products(mp, s, 1))
+                for s in range(2):
+                    r_units.append(lambda mp=mpair, q=idx, t=2 * hf, s=s: add_rb(mp, q, t, s, 1))
             if step == 0:
                 emit_quant(3)
             if step == 3:

@@ -43,7 +43,7 @@ def tile_lorentzmla_pb_kernel(tc, x, freqs_cos, freqs_sin, wq_w, wq_b, out):
     x_rows = x.flatten_outer_dims()
     out_rows = out.rearrange("b s h c -> (b s) (h c)")
     w_pe = wq_w.rearrange("(h r) k -> r h k", r=QK)
-    w_np = wq_w.rearrange("(q a r) k -> a r q k", a=2, r=QK)
+    w_np = wq_w.rearrange("n (a k) -> (n a) k", a=2).rearrange("(h rr) k -> rr h k", rr=2 * QK)
     b_hr = wq_b.rearrange("(o h r) -> o h r", o=1, r=QK)
     cos_src = freqs_cos.rearrange("(t p) j -> p t j", p=P)
     sin_src = freqs_sin.rearrange("(t p) j -> p t j", p=P)
@@ -109,15 +109,14 @@ def tile_lorentzmla_pb_kernel(tc, x, freqs_cos, freqs_sin, wq_w, wq_b, out):
                 return
             kind, idx = CHUNKS[run[1]]
             cols = slice(1024 * run[2], 1024 * (run[2] + 1))
-            dst = raw.rearrange("p (q k) -> p q k", q=4)
             if kind == "P":
+                dst = raw.rearrange("p (q k) -> p q k", q=4)
                 nc.sync.dma_start(out=dst, in_=w_pe[NOPE:QK, 4 * idx : 4 * idx + 4, cols])
             else:
-                for a in range(2):
-                    nc.sync.dma_start(
-                        out=dst[64 * a : 64 * (a + 1), :, :],
-                        in_=w_np[a, 0:NOPE, 4 * idx : 4 * idx + 4, cols],
-                    )
+                dst = raw.rearrange("p (h k) -> p h k", h=8)
+                nc.sync.dma_start(
+                    out=dst, in_=w_np[0 : 2 * NOPE, 8 * idx : 8 * idx + 8, 512 * run[2] : 512 * (run[2] + 1)]
+                )
 
         def emit_run(i, on_vector):
             run = RUNS[i]
@@ -126,6 +125,7 @@ def tile_lorentzmla_pb_kernel(tc, x, freqs_cos, freqs_sin, wq_w, wq_b, out):
             groups[i] = grp
             grp_words = grp.bitcast(F32)
             mat = perm if (run[0] == "w" and CHUNKS[run[1]][0] == "P") else ident
+            split_rows = run[0] == "w" and CHUNKS[run[1]][0] == "N"
             banks = []
             for k in range(4):
                 bank = ps_tr.tile([P, 2, 256], F32, name="trb", tag="trb")
@@ -134,6 +134,8 @@ def tile_lorentzmla_pb_kernel(tc, x, freqs_cos, freqs_sin, wq_w, wq_b, out):
                     for r2 in range(2):
                         if run[0] == "x":
                             start = 1024 * r2 + 256 * k + u
+                        elif split_rows:
+                            start = 256 * (2 * k + r2) + u
                         else:
                             start = 512 * (2 * (k % 2) + r2) + 256 * (k // 2) + u
                         nc.tensor.transpose(
@@ -142,8 +144,12 @@ def tile_lorentzmla_pb_kernel(tc, x, freqs_cos, freqs_sin, wq_w, wq_b, out):
                             mat[:, :],
                         )
             for k in range(4):
-                dst = grp_words[:, 256 * k : 256 * (k + 1), :]
-                src = banks[k].rearrange("p u c -> p c u")
+                if split_rows:
+                    dst = grp_words.rearrange("p (a c) u -> p a c u", a=2)[:, :, 128 * k : 128 * (k + 1), :]
+                    src = banks[k].rearrange("p u (c a) -> p a c u", a=2)
+                else:
+                    dst = grp_words[:, 256 * k : 256 * (k + 1), :]
+                    src = banks[k].rearrange("p u c -> p c u")
                 if k >= 4 - on_vector:
                     nc.vector.tensor_copy(out=dst, in_=src)
                 else:
@@ -190,17 +196,18 @@ def tile_lorentzmla_pb_kernel(tc, x, freqs_cos, freqs_sin, wq_w, wq_b, out):
         def emit_mx(c, tt):
             acc = ps_mx.tile([P, 512], F32, name="acc", tag="acc")
             pair = tt // 2
-            for g in range(4):
+            for slot in range(4):
+                g = slot if CHUNKS[c][0] == "P" else 2 * (slot % 2) + slot // 2
                 xc = slice(256 * g + 128 * (tt % 2), 256 * g + 128 * (tt % 2) + 128)
-                wc = slice(512 * g, 512 * (g + 1))
+                wc = slice(512 * slot, 512 * (slot + 1))
                 nc.tensor.matmul_mx(
                     out=acc[:, :],
                     lhsT=xq[:, pair, xc].bitcast(E5M2X4),
                     lhsT_scale=xs[:, pair, xc],
                     rhs=wcodes[c][:, wc].bitcast(E4M3X4),
                     rhs_scale=wscales[c][:, wc],
-                    start=(g == 0),
-                    stop=(g == 3),
+                    start=(slot == 0),
+                    stop=(slot == 3),
                 )
             return acc
 

@@ -278,6 +278,17 @@ def tile_lorentzmla_pb_kernel(tc, x, freqs_cos, freqs_sin, wq_w, wq_b, out):
             for t in range(t0 + lo, t0 + lo + n):
                 mark(t, quad)
 
+        def add_rb_gpsimd(mpair, quad, t0, s):
+            hs = slice(4 * quad, 4 * quad + 4)
+            mv = mpair.rearrange("p t (h a c) -> p a t h c", a=2, c=ROPE)
+            nc.gpsimd.tensor_tensor(
+                out=o4[:, t0 + s, hs, 1 + NOPE : HEAD_OUT],
+                in0=mv[:, 0, s, :, :],
+                in1=rb[:, s, 512 * quad : 512 * (quad + 1)].rearrange("p (h c) -> p h c", c=ROPE),
+                op=ALU.add,
+            )
+            mark(t0 + s, quad)
+
         def emit_r(n):
             for unused in range(n):
                 if r_pos[0] < len(r_units):
@@ -372,11 +383,14 @@ def tile_lorentzmla_pb_kernel(tc, x, freqs_cos, freqs_sin, wq_w, wq_b, out):
                 else:
                     evac_nope(acc, idx, tt)
                 emit_r(UNITS_AFTER[kind][t2])
-            if kind == "P" and step != n_steps - 1:
+            if kind == "P" and step < n_steps - 2:
                 r_units.append(lambda mp=mpair: sum_products(mp, 0, 2))
                 r_units.append(lambda mp=mpair, q=idx, t=2 * hf: add_rb(mp, q, t, 0, 2))
             if step == n_steps - 2:
                 emit_r(len(r_units))
+                sum_products(mpair, 0, 2)
+                for s in range(2):
+                    add_rb_gpsimd(mpair, idx, 2 * hf, s)
             if step == n_steps - 1:
                 for s in range(2):
                     r_units.append(lambda mp=mpair, s=s: sum_products(mp, s, 1))

@@ -34,7 +34,8 @@ HEAD_RUNS = 4
 RUNS_BEFORE_STEP = {0: (), 1: (4,), 2: (5, 6)}
 WARMUP = 6
 V_EVAC = {"H": 1, "P": 0, "N": 0}
-UNITS_AFTER = {"P": (0, 1), "N": (1, 1)}
+UNITS_AFTER = {"P": (0, 0), "N": (1, 1)}
+UNITS_BEFORE = {"P": 1, "N": 1}
 QUADS_PER_FLUSH = 2
 
 
@@ -94,16 +95,19 @@ def tile_lorentzmla_pb_kernel(tc, x, freqs_cos, freqs_sin, wq_w, wq_b, out):
         ripe = []
         fresh = []
 
-        def emit_load(i):
-            raw = rawp.tile([P, 4096], BF16, name="raw", tag="raw")
-            raws[i] = raw
+        def emit_load(i, quarters=(0, 1, 2, 3)):
+            if i not in raws:
+                raw = rawp.tile([P, 4096], BF16, name="raw", tag="raw")
+                raws[i] = raw
+            raw = raws[i]
             run = RUNS[i]
             if run[0] == "x":
                 dst = raw.rearrange("p (t k) -> p t k", t=2)
                 src = x_rows[256 * run[1] : 256 * (run[1] + 1), :].rearrange("(t p) k -> p t k", p=P)
                 if i == 0:
-                    nc.sync.dma_start(out=dst[:, :, 0:1024], in_=src[:, :, 0:1024])
-                    nc.sync.dma_start(out=dst[:, :, 1024:2048], in_=src[:, :, 1024:2048])
+                    for quarter in quarters:
+                        cols = slice(512 * quarter, 512 * (quarter + 1))
+                        nc.sync.dma_start(out=dst[:, :, cols], in_=src[:, :, cols])
                 else:
                     nc.sync.dma_start(out=dst, in_=src)
                 return
@@ -295,6 +299,7 @@ def tile_lorentzmla_pb_kernel(tc, x, freqs_cos, freqs_sin, wq_w, wq_b, out):
                     r_units[r_pos[0]]()
                     r_pos[0] += 1
 
+        emit_load(0, (0,))
         nc.vector.memset(bt.bitcast(I32), 0)
         nc.vector.memset(brow.bitcast(I32), 0)
         nc.vector.memset(zrhs.bitcast(I32), 0)
@@ -304,7 +309,7 @@ def tile_lorentzmla_pb_kernel(tc, x, freqs_cos, freqs_sin, wq_w, wq_b, out):
         nc.sync.dma_start(out=bt[0:HEADS, :], in_=wq_b.rearrange("(h r) -> h r", r=QK)[:, NOPE:QK])
         nc.sync.dma_start(out=cs[:, :, 0, :], in_=cos_src)
         nc.sync.dma_start(out=cs[:, :, 1, :], in_=sin_src)
-        emit_load(0)
+        emit_load(0, (1, 2, 3))
         nc.sync.dma_start(out=brow[0:1, :].rearrange("p (h n) -> p h n", n=NOPE), in_=b_hr[:, :, 0:NOPE])
         nc.scalar.activation(out=scr_col[:, :], in_=one_col[:, :], func=ACT.Sqrt)
         for i in range(1, RAW_BUFS):
@@ -332,12 +337,13 @@ def tile_lorentzmla_pb_kernel(tc, x, freqs_cos, freqs_sin, wq_w, wq_b, out):
                 nc.tensor.transpose(small[:, 2 + e, :], bt2[:, e, :], ident_b[:, :])
             nc.scalar.copy(out=cs_t[:, :, :], in_=small[:, 0:2, :])
             nc.scalar.copy(out=coef[:, :, :], in_=small[:, 2:4, 0:HEADS].rearrange("p e h -> p h e"))
-            nc.gpsimd.tensor_tensor(
-                out=dmat.rearrange("p (h j e) -> p h j e", j=64, e=2),
-                in0=eye2[:, :].unsqueeze(1).unsqueeze(3).to_broadcast([P, HEADS, 64, 2]),
-                in1=coef[:, :, :].unsqueeze(2).to_broadcast([P, HEADS, 64, 2]),
-                op=ALU.mult,
-            )
+            for quad in range(4):
+                nc.gpsimd.tensor_tensor(
+                    out=dmat[:, 512 * quad : 512 * (quad + 1)].rearrange("p (h j e) -> p h j e", j=64, e=2),
+                    in0=eye2[:, :].unsqueeze(1).unsqueeze(3).to_broadcast([P, 4, 64, 2]),
+                    in1=coef[:, 4 * quad : 4 * quad + 4, :].unsqueeze(2).to_broadcast([P, 4, 64, 2]),
+                    op=ALU.mult,
+                )
             nc.vector.tensor_copy(out=tab1[:, :, 0, :, 0], in_=cs[:, :, 0, :])
             nc.vector.tensor_copy(out=tab1[:, :, 0, :, 1], in_=cs[:, :, 1, :])
             nc.vector.tensor_scalar_mul(out=tab1[:, :, 1, :, 0], in0=cs[:, :, 1, :], scalar1=-1.0)
@@ -349,13 +355,13 @@ def tile_lorentzmla_pb_kernel(tc, x, freqs_cos, freqs_sin, wq_w, wq_b, out):
 
         emit_tables()
         emit_run(0, V_EVAC["H"])
-        emit_dummies(2)
+        emit_bias_np()
         emit_quant(0)
         emit_run(1, V_EVAC["H"])
         emit_rb(0)
         emit_quant(1)
         emit_run(2, V_EVAC["H"])
-        emit_bias_np()
+        emit_rb(1)
         emit_quant(2)
         emit_run(3, V_EVAC["H"])
 
@@ -368,10 +374,13 @@ def tile_lorentzmla_pb_kernel(tc, x, freqs_cos, freqs_sin, wq_w, wq_b, out):
             todo = [i for i in runs if i < N_RUNS]
             for n, i in enumerate(todo):
                 if n > 0:
-                    emit_rb(1)
+                    emit_rb(2)
                 emit_run(i, V_EVAC[kind])
             flush_scalar(QUADS_PER_FLUSH)
-            for i in todo:
+            emit_r(UNITS_BEFORE[kind])
+            for n, i in enumerate(todo):
+                if n > 0:
+                    emit_r(2)
                 emit_quant(i)
             if kind == "P":
                 mpair = mpool.tile([P, 2, 1024], F32, name="mpair", tag="mpair")
@@ -399,8 +408,6 @@ def tile_lorentzmla_pb_kernel(tc, x, freqs_cos, freqs_sin, wq_w, wq_b, out):
             if step == 0:
                 emit_quant(3)
             if step == 3:
-                emit_rb(2)
-            if step == 4:
                 emit_rb(3)
         while r_pos[0] < len(r_units):
             emit_r(1)

@@ -79,8 +79,8 @@ def tile_lorentzmla_pb_kernel(tc, x, freqs_cos, freqs_sin, wq_w, wq_b, out):
         b_np = const.tile([P, HEADS * NOPE], F32, name="b_np")
         one_col = const.tile([P, 1], F32, name="one_col")
         scr_col = const.tile([P, 1], F32, name="scr_col")
-        xq = const.tile([P, 2, 1024], U32, name="xq", align_bytes=64)
-        xs = const.tile([P, 2, 1024], U8, name="xs", align_bytes=64)
+        xq = const.tile([P, 2, 1024], U32, name="xq", align_bytes=256)
+        xs = const.tile([P, 2, 1024], U8, name="xs", align_bytes=256)
         tot = const.tile([P, 4, HEADS], F32, name="tot")
         o_all = const.tile([P, 4, OUT_COLS], F32, name="o_all")
         o4 = o_all.rearrange("p t (h c) -> p t h c", c=HEAD_OUT)
@@ -125,7 +125,7 @@ def tile_lorentzmla_pb_kernel(tc, x, freqs_cos, freqs_sin, wq_w, wq_b, out):
         def emit_run(i, on_vector):
             run = RUNS[i]
             words = raws[i].bitcast(F32)
-            grp = grpp.tile([P, 1024, 4], BF16, name="grp", tag="grp", align_bytes=64)
+            grp = grpp.tile([P, 1024, 4], BF16, name="grp", tag="grp", align_bytes=256)
             groups[i] = grp
             grp_words = grp.bitcast(F32)
             mat = perm if (run[0] == "w" and CHUNKS[run[1]][0] == "P") else ident
@@ -169,8 +169,8 @@ def tile_lorentzmla_pb_kernel(tc, x, freqs_cos, freqs_sin, wq_w, wq_b, out):
                 return
             c = run[1]
             if run[2] == 0:
-                wq = codep.tile([P, 2048], U32, name="wq", tag="wq", align_bytes=64)
-                ws = codep.tile([P, 2048], U8, name="ws", tag="ws", align_bytes=64)
+                wq = codep.tile([P, 2048], U32, name="wq", tag="wq", align_bytes=256)
+                ws = codep.tile([P, 2048], U8, name="ws", tag="ws", align_bytes=256)
                 wcodes[c] = wq
                 wscales[c] = ws
             cols = slice(1024 * run[2], 1024 * (run[2] + 1))

@@ -37,6 +37,7 @@ V_EVAC = {"H": 1, "P": 0, "N": 0}
 UNITS_AFTER = {"P": (0, 0), "N": (1, 1)}
 UNITS_BEFORE = {"P": 1, "N": 1}
 QUADS_PER_FLUSH = 2
+V_LAST_SQUARES = 3
 
 
 def tile_lorentzmla_pb_kernel(tc, x, freqs_cos, freqs_sin, wq_w, wq_b, out):
@@ -45,7 +46,6 @@ def tile_lorentzmla_pb_kernel(tc, x, freqs_cos, freqs_sin, wq_w, wq_b, out):
     out_rows = out.rearrange("b s h c -> (b s) (h c)")
     w_pe = wq_w.rearrange("(h r) k -> r h k", r=QK)
     w_np = wq_w.rearrange("n (a k) -> (n a) k", a=2).rearrange("(h rr) k -> rr h k", rr=2 * QK)
-    b_hr = wq_b.rearrange("(o h r) -> o h r", o=1, r=QK)
     cos_src = freqs_cos.rearrange("(t p) j -> p t j", p=P)
     sin_src = freqs_sin.rearrange("(t p) j -> p t j", p=P)
 
@@ -63,7 +63,6 @@ def tile_lorentzmla_pb_kernel(tc, x, freqs_cos, freqs_sin, wq_w, wq_b, out):
         ident = const.tile([P, P], F32, name="ident")
         perm = const.tile([P, P], F32, name="perm")
         ident_b = const.tile([P, P], BF16, name="ident_b")
-        ones_b = const.tile([P, P], BF16, name="ones_b")
         eye2 = const.tile([P, 64], BF16, name="eye2")
         zrhs = const.tile([P, 512], BF16, name="zrhs")
         cs = const.tile([P, 2, 2, 64], BF16, name="cs")
@@ -75,8 +74,7 @@ def tile_lorentzmla_pb_kernel(tc, x, freqs_cos, freqs_sin, wq_w, wq_b, out):
         coef = const.tile([P, HEADS, 2], BF16, name="coef")
         dmat = const.tile([P, HEADS * ROPE], BF16, name="dmat")
         rb = const.tile([P, 2, HEADS * ROPE], F32, name="rb")
-        brow = const.tile([P, HEADS * NOPE], BF16, name="brow")
-        b_np = const.tile([P, HEADS * NOPE], F32, name="b_np")
+        b_all = const.tile([P, HEADS * QK], BF16, name="b_all")
         one_col = const.tile([P, 1], F32, name="one_col")
         scr_col = const.tile([P, 1], F32, name="scr_col")
         xq = const.tile([P, 2, 1024], U32, name="xq", align_bytes=256)
@@ -183,13 +181,6 @@ def tile_lorentzmla_pb_kernel(tc, x, freqs_cos, freqs_sin, wq_w, wq_b, out):
             for unused in range(n):
                 nc.tensor.matmul(bank[:, :], lhsT=ident_b[:, :], rhs=zrhs[:, :], start=True, stop=True)
 
-        def emit_bias_np():
-            for k in range(2):
-                bank = ps_mx.tile([P, 512], F32, name="acc", tag="acc")
-                cols = slice(512 * k, 512 * (k + 1))
-                nc.tensor.matmul(bank[:, :], lhsT=ones_b[:, :], rhs=brow[:, cols], start=True, stop=True)
-                nc.scalar.copy(out=b_np[:, cols], in_=bank[:, :])
-
         def emit_rb(quad):
             for st in range(2):
                 bank = ps_mx.tile([P, 512], F32, name="acc", tag="acc")
@@ -217,7 +208,15 @@ def tile_lorentzmla_pb_kernel(tc, x, freqs_cos, freqs_sin, wq_w, wq_b, out):
 
         def finish_quad(tt, quad):
             hs = slice(4 * quad, 4 * quad + 4)
+            last = tt == 3 and quad == 3
             for h in range(4 * quad, 4 * quad + 4):
+                if last and h >= 4 * quad + 4 - V_LAST_SQUARES:
+                    vjunk = junkp.tile([P, QK], F32, name="vjunk", tag="vjunk")
+                    nc.vector.scalar_tensor_tensor(
+                        out=vjunk[:, :], in0=o4[:, tt, h, 1:HEAD_OUT], scalar=1.0, in1=o4[:, tt, h, 1:HEAD_OUT],
+                        op0=ALU.mult, op1=ALU.mult, accum_out=tot[:, tt, h : h + 1],
+                    )
+                    continue
                 junk = junkp.tile([P, QK], F32, name="junk", tag="junk")
                 nc.scalar.activation(
                     out=junk[:, :], in_=o4[:, tt, h, 1:HEAD_OUT], func=ACT.Square, accum_out=tot[:, tt, h : h + 1]
@@ -248,7 +247,7 @@ def tile_lorentzmla_pb_kernel(tc, x, freqs_cos, freqs_sin, wq_w, wq_b, out):
             nc.vector.tensor_tensor(
                 out=o4[:, tt, hs, 1 : 1 + NOPE],
                 in0=acc.rearrange("p (h n) -> p h n", n=NOPE),
-                in1=b_np[:, 512 * half : 512 * (half + 1)].rearrange("p (h n) -> p h n", n=NOPE),
+                in1=b_all.rearrange("p (h r) -> p h r", r=QK)[:, hs, 0:NOPE],
                 op=ALU.add,
             )
             mark(tt, 2 * half)
@@ -301,19 +300,17 @@ def tile_lorentzmla_pb_kernel(tc, x, freqs_cos, freqs_sin, wq_w, wq_b, out):
 
         emit_load(0, (0,))
         nc.vector.memset(bt.bitcast(I32), 0)
-        nc.vector.memset(brow.bitcast(I32), 0)
         nc.vector.memset(zrhs.bitcast(I32), 0)
-        nc.vector.memset(ones_b[:, :], 1.0)
         nc.vector.memset(one_col[:, :], 1.0)
         make_identity(nc, ident[:, :])
         nc.sync.dma_start(out=bt[0:HEADS, :], in_=wq_b.rearrange("(h r) -> h r", r=QK)[:, NOPE:QK])
         nc.sync.dma_start(out=cs[:, :, 0, :], in_=cos_src)
         nc.sync.dma_start(out=cs[:, :, 1, :], in_=sin_src)
         emit_load(0, (1, 2, 3))
-        nc.sync.dma_start(out=brow[0:1, :].rearrange("p (h n) -> p h n", n=NOPE), in_=b_hr[:, :, 0:NOPE])
         nc.scalar.activation(out=scr_col[:, :], in_=one_col[:, :], func=ACT.Sqrt)
         for i in range(1, RAW_BUFS):
             emit_load(i)
+        nc.sync.dma_start(out=b_all[:, :], in_=wq_b.partition_broadcast(P))
 
         nc.vector.tensor_copy(out=ident_b[:, :], in_=ident[:, :])
         emit_dummies(WARMUP)
@@ -355,7 +352,6 @@ def tile_lorentzmla_pb_kernel(tc, x, freqs_cos, freqs_sin, wq_w, wq_b, out):
 
         emit_tables()
         emit_run(0, V_EVAC["H"])
-        emit_bias_np()
         emit_quant(0)
         emit_run(1, V_EVAC["H"])
         emit_rb(0)

@@ -206,8 +206,7 @@ def tile_lorentzmla_pb_kernel(tc, x, freqs_cos, freqs_sin, wq_w, wq_b, out):
                 )
             return acc
 
-        def finish_quad(tt, quad):
-            hs = slice(4 * quad, 4 * quad + 4)
+        def square_quad(tt, quad):
             last = tt == 3 and quad == 3
             for h in range(4 * quad, 4 * quad + 4):
                 if last and h >= 4 * quad + 4 - V_LAST_SQUARES:
@@ -221,9 +220,8 @@ def tile_lorentzmla_pb_kernel(tc, x, freqs_cos, freqs_sin, wq_w, wq_b, out):
                 nc.scalar.activation(
                     out=junk[:, :], in_=o4[:, tt, h, 1:HEAD_OUT], func=ACT.Square, accum_out=tot[:, tt, h : h + 1]
                 )
-            nc.scalar.activation(
-                out=o4[:, tt, hs, 0:1], in_=tot[:, tt, hs].unsqueeze(2), func=ACT.Sqrt, bias=one_col[:, 0:1]
-            )
+
+        def store_quad(tt, quad):
             base = HALF_COLS * (quad // 2)
             lo = base + 768 * (quad % 2)
             hi = base + (768 if quad % 2 == 0 else HALF_COLS)
@@ -234,11 +232,39 @@ def tile_lorentzmla_pb_kernel(tc, x, freqs_cos, freqs_sin, wq_w, wq_b, out):
             if written[(tt, quad)] == 2:
                 fresh.append((tt, quad))
 
-        def flush_scalar(n):
-            for unused in range(n):
-                if ripe:
-                    tt, quad = ripe.pop(0)
-                    finish_quad(tt, quad)
+        def flush_scalar(n, share_root=False):
+            taken = [ripe.pop(0) for unused in range(min(n, len(ripe)))]
+            if not share_root:
+                for tt, quad in taken:
+                    hs = slice(4 * quad, 4 * quad + 4)
+                    square_quad(tt, quad)
+                    nc.scalar.activation(
+                        out=o4[:, tt, hs, 0:1], in_=tot[:, tt, hs].unsqueeze(2), func=ACT.Sqrt, bias=1.0
+                    )
+                    store_quad(tt, quad)
+                ripe.extend(fresh)
+                fresh.clear()
+                return
+            for tt, quad in taken:
+                square_quad(tt, quad)
+            if len(taken) == 2 and taken[0][0] == taken[1][0] and taken[0][1] + 1 == taken[1][1]:
+                tt, quad = taken[0]
+                hs = slice(4 * quad, 4 * quad + 8)
+                nc.scalar.activation(out=o4[:, tt, hs, 0:1], in_=tot[:, tt, hs].unsqueeze(2), func=ACT.Sqrt, bias=1.0)
+            elif len(taken) == 2 and taken[0][1] == taken[1][1] and taken[0][0] + 1 == taken[1][0]:
+                tt, quad = taken[0]
+                hs = slice(4 * quad, 4 * quad + 4)
+                nc.scalar.activation(
+                    out=o4[:, tt : tt + 2, hs, 0:1], in_=tot[:, tt : tt + 2, hs].unsqueeze(3), func=ACT.Sqrt, bias=1.0
+                )
+            else:
+                for tt, quad in taken:
+                    hs = slice(4 * quad, 4 * quad + 4)
+                    nc.scalar.activation(
+                        out=o4[:, tt, hs, 0:1], in_=tot[:, tt, hs].unsqueeze(2), func=ACT.Sqrt, bias=1.0
+                    )
+            for tt, quad in taken:
+                store_quad(tt, quad)
             ripe.extend(fresh)
             fresh.clear()
 
@@ -372,7 +398,7 @@ def tile_lorentzmla_pb_kernel(tc, x, freqs_cos, freqs_sin, wq_w, wq_b, out):
                 if n > 0:
                     emit_rb(2)
                 emit_run(i, V_EVAC[kind])
-            flush_scalar(QUADS_PER_FLUSH)
+            flush_scalar(QUADS_PER_FLUSH, share_root=True)
             emit_r(UNITS_BEFORE[kind])
             for n, i in enumerate(todo):
                 if n > 0:

@@ -55,7 +55,7 @@ def tile_lorentzmla_pb_kernel(tc, x, freqs_cos, freqs_sin, wq_w, wq_b, out):
         grpp = ctx.enter_context(tc.tile_pool(name="grpp", bufs=3))
         codep = ctx.enter_context(tc.tile_pool(name="codep", bufs=3))
         mpool = ctx.enter_context(tc.tile_pool(name="mpool", bufs=5))
-        junkp = ctx.enter_context(tc.tile_pool(name="junkp", bufs=2))
+        junkp = ctx.enter_context(tc.tile_pool(name="junkp", bufs=4))
         ps_tr = ctx.enter_context(tc.psum_pool(name="ps_tr", bufs=4))
         ps_mx = ctx.enter_context(tc.psum_pool(name="ps_mx", bufs=4))
         ctx.enter_context(tc.manual_schedule())
@@ -92,6 +92,7 @@ def tile_lorentzmla_pb_kernel(tc, x, freqs_cos, freqs_sin, wq_w, wq_b, out):
         written = {}
         ripe = []
         fresh = []
+        squared = []
 
         def emit_load(i, quarters=(0, 1, 2, 3)):
             if i not in raws:
@@ -232,41 +233,37 @@ def tile_lorentzmla_pb_kernel(tc, x, freqs_cos, freqs_sin, wq_w, wq_b, out):
             if written[(tt, quad)] == 2:
                 fresh.append((tt, quad))
 
-        def flush_scalar(n, share_root=False):
-            taken = [ripe.pop(0) for unused in range(min(n, len(ripe)))]
-            if not share_root:
-                for tt, quad in taken:
-                    hs = slice(4 * quad, 4 * quad + 4)
-                    square_quad(tt, quad)
-                    nc.scalar.activation(
-                        out=o4[:, tt, hs, 0:1], in_=tot[:, tt, hs].unsqueeze(2), func=ACT.Sqrt, bias=1.0
-                    )
-                    store_quad(tt, quad)
-                ripe.extend(fresh)
-                fresh.clear()
-                return
-            for tt, quad in taken:
-                square_quad(tt, quad)
-            if len(taken) == 2 and taken[0][0] == taken[1][0] and taken[0][1] + 1 == taken[1][1]:
-                tt, quad = taken[0]
-                hs = slice(4 * quad, 4 * quad + 8)
-                nc.scalar.activation(out=o4[:, tt, hs, 0:1], in_=tot[:, tt, hs].unsqueeze(2), func=ACT.Sqrt, bias=1.0)
-            elif len(taken) == 2 and taken[0][1] == taken[1][1] and taken[0][0] + 1 == taken[1][0]:
-                tt, quad = taken[0]
-                hs = slice(4 * quad, 4 * quad + 4)
-                nc.scalar.activation(
-                    out=o4[:, tt : tt + 2, hs, 0:1], in_=tot[:, tt : tt + 2, hs].unsqueeze(3), func=ACT.Sqrt, bias=1.0
-                )
+        def root(tt0, n_tt, h0, n_h):
+            nc.scalar.activation(
+                out=o4[:, tt0 : tt0 + n_tt, h0 : h0 + n_h, 0:1],
+                in_=tot[:, tt0 : tt0 + n_tt, h0 : h0 + n_h].unsqueeze(3),
+                func=ACT.Sqrt,
+                bias=1.0,
+            )
+
+        def roots_and_stores(groups):
+            if len(groups) == 2 and groups[0][0] == groups[1][0] and groups[0][1] + 1 == groups[1][1]:
+                root(groups[0][0], 1, 4 * groups[0][1], 8)
+            elif len(groups) == 2 and groups[0][1] == groups[1][1] and groups[0][0] + 1 == groups[1][0]:
+                root(groups[0][0], 2, 4 * groups[0][1], 4)
             else:
-                for tt, quad in taken:
-                    hs = slice(4 * quad, 4 * quad + 4)
-                    nc.scalar.activation(
-                        out=o4[:, tt, hs, 0:1], in_=tot[:, tt, hs].unsqueeze(2), func=ACT.Sqrt, bias=1.0
-                    )
-            for tt, quad in taken:
+                for tt, quad in groups:
+                    root(tt, 1, 4 * quad, 4)
+            for tt, quad in groups:
                 store_quad(tt, quad)
+
+        def flush_scalar(n):
             ripe.extend(fresh)
             fresh.clear()
+            roots_and_stores(squared)
+            squared.clear()
+            for unused in range(min(n, len(ripe))):
+                tt, quad = ripe.pop(0)
+                square_quad(tt, quad)
+                if quad == 3:
+                    roots_and_stores([(tt, quad)])
+                else:
+                    squared.append((tt, quad))
 
         def evac_nope(acc, half, tt):
             hs = slice(8 * half, 8 * half + 8)
@@ -398,7 +395,7 @@ def tile_lorentzmla_pb_kernel(tc, x, freqs_cos, freqs_sin, wq_w, wq_b, out):
                 if n > 0:
                     emit_rb(2)
                 emit_run(i, V_EVAC[kind])
-            flush_scalar(QUADS_PER_FLUSH, share_root=True)
+            flush_scalar(QUADS_PER_FLUSH)
             emit_r(UNITS_BEFORE[kind])
             for n, i in enumerate(todo):
                 if n > 0:
@@ -433,7 +430,5 @@ def tile_lorentzmla_pb_kernel(tc, x, freqs_cos, freqs_sin, wq_w, wq_b, out):
                 emit_rb(3)
         while r_pos[0] < len(r_units):
             emit_r(1)
-            flush_scalar(0)
             flush_scalar(2)
-        flush_scalar(4)
         flush_scalar(4)

@@ -38,6 +38,7 @@ UNITS_AFTER = {"P": (0, 0), "N": (1, 1)}
 UNITS_BEFORE = {"P": 1, "N": 1}
 QUADS_PER_FLUSH = 2
 V_LAST_SQUARES = 3
+GROUPS_PER_ROOT = 4
 
 
 def tile_lorentzmla_pb_kernel(tc, x, freqs_cos, freqs_sin, wq_w, wq_b, out):
@@ -242,21 +243,21 @@ def tile_lorentzmla_pb_kernel(tc, x, freqs_cos, freqs_sin, wq_w, wq_b, out):
             )
 
         def roots_and_stores(groups):
-            if len(groups) == 2 and groups[0][0] == groups[1][0] and groups[0][1] + 1 == groups[1][1]:
-                root(groups[0][0], 1, 4 * groups[0][1], 8)
-            elif len(groups) == 2 and groups[0][1] == groups[1][1] and groups[0][0] + 1 == groups[1][0]:
-                root(groups[0][0], 2, 4 * groups[0][1], 4)
-            else:
-                for tt, quad in groups:
-                    root(tt, 1, 4 * quad, 4)
+            tts = sorted(set(tt for tt, quad in groups))
+            quads = sorted(set(quad for tt, quad in groups))
+            if groups:
+                assert len(groups) == len(tts) * len(quads)
+                assert tts[-1] - tts[0] + 1 == len(tts) and quads[-1] - quads[0] + 1 == len(quads)
+                root(tts[0], len(tts), 4 * quads[0], 4 * len(quads))
             for tt, quad in groups:
                 store_quad(tt, quad)
 
         def flush_scalar(n):
             ripe.extend(fresh)
             fresh.clear()
-            roots_and_stores(squared)
-            squared.clear()
+            if len(squared) >= GROUPS_PER_ROOT or not ripe or ripe[0][1] == 3:
+                roots_and_stores(squared)
+                squared.clear()
             for unused in range(min(n, len(ripe))):
                 tt, quad = ripe.pop(0)
                 square_quad(tt, quad)

from contextlib import ExitStack

import concourse.mybir as mybir
from concourse.masks import make_identity

F32 = mybir.dt.float32
BF16 = mybir.dt.bfloat16
I32 = mybir.dt.int32
U32 = mybir.dt.uint32
U8 = mybir.dt.uint8
E5M2X4 = mybir.dt.float8_e5m2_x4
E4M3X4 = mybir.dt.float8_e4m3fn_x4
ALU = mybir.AluOpType
ACT = mybir.ActivationFunctionType

P = 128
TOKENS = 512
DIM = 2048
HEADS = 16
NOPE = 64
ROPE = 128
QK = NOPE + ROPE
HEAD_OUT = QK + 1
OUT_COLS = HEADS * HEAD_OUT
HALF_COLS = 8 * HEAD_OUT

FLOPS = 2 * TOKENS * HEADS * QK * DIM

CHUNKS = (("P", 0), ("P", 1), ("N", 0), ("P", 2), ("N", 1), ("P", 3))
RUNS = (("x", 0), ("w", 0, 0), ("w", 0, 1), ("x", 1)) + tuple(("w", c, hf) for c in range(1, 6) for hf in range(2))
N_RUNS = len(RUNS)
RAW_BUFS = 5
HEAD_RUNS = 4
RUNS_BEFORE_STEP = {0: (), 1: (4,), 2: (5, 6)}
WARMUP = 6
V_EVAC = {"H": 1, "P": 0, "N": 0}
UNITS_AFTER = {"P": (0, 0), "N": (1, 1)}
UNITS_BEFORE = {"P": 1, "N": 1}
QUADS_PER_FLUSH = 2
V_LAST_SQUARES = 3
GROUPS_PER_ROOT = 4


def tile_lorentzmla_pb_kernel(tc, x, freqs_cos, freqs_sin, wq_w, wq_b, out):
    nc = tc.nc
    x_rows = x.flatten_outer_dims()
    out_rows = out.rearrange("b s h c -> (b s) (h c)")
    w_pe = wq_w.rearrange("(h r) k -> r h k", r=QK)
    w_np = wq_w.rearrange("n (a k) -> (n a) k", a=2).rearrange("(h rr) k -> rr h k", rr=2 * QK)
    cos_src = freqs_cos.rearrange("(t p) j -> p t j", p=P)
    sin_src = freqs_sin.rearrange("(t p) j -> p t j", p=P)

    with ExitStack() as ctx:
        const = ctx.enter_context(tc.tile_pool(name="const", bufs=1))
        rawp = ctx.enter_context(tc.tile_pool(name="rawp", bufs=RAW_BUFS))
        grpp = ctx.enter_context(tc.tile_pool(name="grpp", bufs=3))
        codep = ctx.enter_context(tc.tile_pool(name="codep", bufs=3))
        mpool = ctx.enter_context(tc.tile_pool(name="mpool", bufs=5))
        junkp = ctx.enter_context(tc.tile_pool(name="junkp", bufs=4))
        ps_tr = ctx.enter_context(tc.psum_pool(name="ps_tr", bufs=4))
        ps_mx = ctx.enter_context(tc.psum_pool(name="ps_mx", bufs=4))
        ctx.enter_context(tc.manual_schedule())

        ident = const.tile([P, P], F32, name="ident")
        perm = const.tile([P, P], F32, name="perm")
        ident_b = const.tile([P, P], BF16, name="ident_b")
        eye2 = const.tile([P, 64], BF16, name="eye2")
        zrhs = const.tile([P, 512], BF16, name="zrhs")
        cs = const.tile([P, 2, 2, 64], BF16, name="cs")
        tab1 = const.tile([P, 2, 2, 64, 2], BF16, name="tab1")
        tabf = const.tile([P, 2, 4, 256], BF16, name="tabf")
        cs_t = const.tile([P, 2, P], BF16, name="cs_t")
        bt = const.tile([P, P], BF16, name="bt")
        bt2 = const.tile([P, 2, P], BF16, name="bt2")
        coef = const.tile([P, HEADS, 2], BF16, name="coef")
        dmat = const.tile([P, HEADS * ROPE], BF16, name="dmat")
        rb = const.tile([P, 2, HEADS * ROPE], F32, name="rb")
        b_all = const.tile([P, HEADS * QK], BF16, name="b_all")
        one_col = const.tile([P, 1], F32, name="one_col")
        scr_col = const.tile([P, 1], F32, name="scr_col")
        xq = const.tile([P, 2, 1024], U32, name="xq", align_bytes=256)
        xs = const.tile([P, 2, 1024], U8, name="xs", align_bytes=256)
        tot = const.tile([P, 4, HEADS], F32, name="tot")
        o_all = const.tile([P, 4, OUT_COLS], F32, name="o_all")
        o4 = o_all.rearrange("p t (h c) -> p t h c", c=HEAD_OUT)

        raws = {}
        groups = {}
        wcodes = {}
        wscales = {}
        r_units = []
        r_pos = [0]
        written = {}
        ripe = []
        fresh = []
        squared = []

        def emit_load(i, quarters=(0, 1, 2, 3)):
            if i not in raws:
                raw = rawp.tile([P, 4096], BF16, name="raw", tag="raw")
                raws[i] = raw
            raw = raws[i]
            run = RUNS[i]
            if run[0] == "x":
                dst = raw.rearrange("p (t k) -> p t k", t=2)
                src = x_rows[256 * run[1] : 256 * (run[1] + 1), :].rearrange("(t p) k -> p t k", p=P)
                if i == 0:
                    for quarter in quarters:
                        cols = slice(512 * quarter, 512 * (quarter + 1))
                        nc.sync.dma_start(out=dst[:, :, cols], in_=src[:, :, cols])
                else:
                    nc.sync.dma_start(out=dst, in_=src)
                return
            kind, idx = CHUNKS[run[1]]
            cols = slice(1024 * run[2], 1024 * (run[2] + 1))
            if kind == "P":
                dst = raw.rearrange("p (q k) -> p q k", q=4)
                nc.sync.dma_start(out=dst, in_=w_pe[NOPE:QK, 4 * idx : 4 * idx + 4, cols])
            else:
                dst = raw.rearrange("p (h k) -> p h k", h=8)
                nc.sync.dma_start(
                    out=dst, in_=w_np[0 : 2 * NOPE, 8 * idx : 8 * idx + 8, 512 * run[2] : 512 * (run[2] + 1)]
                )

        def emit_run(i, on_vector):
            run = RUNS[i]
            words = raws[i].bitcast(F32)
            grp = grpp.tile([P, 1024, 4], BF16, name="grp", tag="grp", align_bytes=256)
            groups[i] = grp
            grp_words = grp.bitcast(F32)
            mat = perm if (run[0] == "w" and CHUNKS[run[1]][0] == "P") else ident
            split_rows = run[0] == "w" and CHUNKS[run[1]][0] == "N"
            banks = []
            for k in range(4):
                bank = ps_tr.tile([P, 2, 256], F32, name="trb", tag="trb")
                banks.append(bank)
                for u in range(2):
                    for r2 in range(2):
                        if run[0] == "x":
                            start = 1024 * r2 + 256 * k + u
                        elif split_rows:
                            start = 256 * (2 * k + r2) + u
                        else:
                            start = 512 * (2 * (k % 2) + r2) + 256 * (k // 2) + u
                        nc.tensor.transpose(
                            bank[:, u, 128 * r2 : 128 * (r2 + 1)],
                            words[:, start : start + 255 : 2],
                            mat[:, :],
                        )
            for k in range(4):
                if split_rows:
                    dst = grp_words.rearrange("p (a c) u -> p a c u", a=2)[:, :, 128 * k : 128 * (k + 1), :]
                    src = banks[k].rearrange("p u (c a) -> p a c u", a=2)
                else:
                    dst = grp_words[:, 256 * k : 256 * (k + 1), :]
                    src = banks[k].rearrange("p u c -> p c u")
                if k >= 4 - on_vector:
                    nc.vector.tensor_copy(out=dst, in_=src)
                else:
                    nc.scalar.copy(out=dst, in_=src)
            if i + RAW_BUFS < N_RUNS:
                emit_load(i + RAW_BUFS)

        def emit_quant(i):
            run = RUNS[i]
            flat = groups[i].rearrange("p c t -> p (c t)")
            if run[0] == "x":
                nc.vector.quantize_mx(out=xq[:, run[1], :].bitcast(E5M2X4), scales=xs[:, run[1], :], in_=flat)
                return
            c = run[1]
            if run[2] == 0:
                wq = codep.tile([P, 2048], U32, name="wq", tag="wq", align_bytes=256)
                ws = codep.tile([P, 2048], U8, name="ws", tag="ws", align_bytes=256)
                wcodes[c] = wq
                wscales[c] = ws
            cols = slice(1024 * run[2], 1024 * (run[2] + 1))
            nc.vector.quantize_mx(
                out=wcodes[c][:, cols].bitcast(E4M3X4), scales=wscales[c][:, cols], in_=flat
            )

        def emit_dummies(n):
            bank = ps_mx.tile([P, 512], F32, name="acc", tag="acc")
            for unused in range(n):
                nc.tensor.matmul(bank[:, :], lhsT=ident_b[:, :], rhs=zrhs[:, :], start=True, stop=True)

        def emit_rb(quad):
            for st in range(2):
                bank = ps_mx.tile([P, 512], F32, name="acc", tag="acc")
                cols = slice(512 * quad, 512 * (quad + 1))
                nc.tensor.matmul(bank[:, :], lhsT=cs_t[:, st, :], rhs=dmat[:, cols], start=True, stop=True)
                nc.scalar.copy(out=rb[:, st, cols], in_=bank[:, :])

        def emit_mx(c, tt):
            acc = ps_mx.tile([P, 512], F32, name="acc", tag="acc")
            pair = tt // 2
            for slot in range(4):
                g = slot if CHUNKS[c][0] == "P" else 2 * (slot % 2) + slot // 2
                xc = slice(256 * g + 128 * (tt % 2), 256 * g + 128 * (tt % 2) + 128)
                wc = slice(512 * slot, 512 * (slot + 1))
                nc.tensor.matmul_mx(
                    out=acc[:, :],
                    lhsT=xq[:, pair, xc].bitcast(E5M2X4),
                    lhsT_scale=xs[:, pair, xc],
                    rhs=wcodes[c][:, wc].bitcast(E4M3X4),
                    rhs_scale=wscales[c][:, wc],
                    start=(slot == 0),
                    stop=(slot == 3),
                )
            return acc

        def square_quad(tt, quad):
            last = tt == 3 and quad == 3
            for h in range(4 * quad, 4 * quad + 4):
                if last and h >= 4 * quad + 4 - V_LAST_SQUARES:
                    vjunk = junkp.tile([P, QK], F32, name="vjunk", tag="vjunk")
                    nc.vector.scalar_tensor_tensor(
                        out=vjunk[:, :], in0=o4[:, tt, h, 1:HEAD_OUT], scalar=1.0, in1=o4[:, tt, h, 1:HEAD_OUT],
                        op0=ALU.mult, op1=ALU.mult, accum_out=tot[:, tt, h : h + 1],
                    )
                    continue
                junk = junkp.tile([P, QK], F32, name="junk", tag="junk")
                nc.scalar.activation(
                    out=junk[:, :], in_=o4[:, tt, h, 1:HEAD_OUT], func=ACT.Square, accum_out=tot[:, tt, h : h + 1]
                )

        def store_quad(tt, quad):
            base = HALF_COLS * (quad // 2)
            lo = base + 768 * (quad % 2)
            hi = base + (768 if quad % 2 == 0 else HALF_COLS)
            nc.sync.dma_start(out=out_rows[P * tt : P * (tt + 1), lo:hi], in_=o_all[:, tt, lo:hi])

        def mark(tt, quad):
            written[(tt, quad)] = written.get((tt, quad), 0) + 1
            if written[(tt, quad)] == 2:
                fresh.append((tt, quad))

        def root(tt0, n_tt, h0, n_h):
            nc.scalar.activation(
                out=o4[:, tt0 : tt0 + n_tt, h0 : h0 + n_h, 0:1],
                in_=tot[:, tt0 : tt0 + n_tt, h0 : h0 + n_h].unsqueeze(3),
                func=ACT.Sqrt,
                bias=1.0,
            )

        def roots_and_stores(groups):
            tts = sorted(set(tt for tt, quad in groups))
            quads = sorted(set(quad for tt, quad in groups))
            if groups:
                assert len(groups) == len(tts) * len(quads)
                assert tts[-1] - tts[0] + 1 == len(tts) and quads[-1] - quads[0] + 1 == len(quads)
                root(tts[0], len(tts), 4 * quads[0], 4 * len(quads))
            for tt, quad in groups:
                store_quad(tt, quad)

        def flush_scalar(n):
            ripe.extend(fresh)
            fresh.clear()
            if len(squared) >= GROUPS_PER_ROOT or not ripe or ripe[0][1] == 3:
                roots_and_stores(squared)
                squared.clear()
            for unused in range(min(n, len(ripe))):
                tt, quad = ripe.pop(0)
                square_quad(tt, quad)
                if quad == 3:
                    roots_and_stores([(tt, quad)])
                else:
                    squared.append((tt, quad))

        def evac_nope(acc, half, tt):
            hs = slice(8 * half, 8 * half + 8)
            nc.vector.tensor_tensor(
                out=o4[:, tt, hs, 1 : 1 + NOPE],
                in0=acc.rearrange("p (h n) -> p h n", n=NOPE),
                in1=b_all.rearrange("p (h r) -> p h r", r=QK)[:, hs, 0:NOPE],
                op=ALU.add,
            )
            mark(tt, 2 * half)
            mark(tt, 2 * half + 1)

        def products(acc, tt, mpair):
            st = tt % 2
            nc.vector.tensor_tensor(
                out=mpair[:, st, :].rearrange("p (g j e) -> p g j e", j=64, e=2),
                in0=acc.rearrange("p (g j) -> p g j", j=64).unsqueeze(3).to_broadcast([P, 8, 64, 2]),
                in1=tabf[:, st, :, :].rearrange("p h (a j e) -> p (h a) j e", j=64, e=2),
                op=ALU.mult,
            )

        def sum_products(mpair, lo, n):
            mv = mpair.rearrange("p t (h a c) -> p a t h c", a=2, c=ROPE)
            nc.vector.tensor_tensor(
                out=mv[:, 0, lo : lo + n, :, :], in0=mv[:, 0, lo : lo + n, :, :], in1=mv[:, 1, lo : lo + n, :, :],
                op=ALU.add,
            )

        def add_rb(mpair, quad, t0, lo, n):
            hs = slice(4 * quad, 4 * quad + 4)
            mv = mpair.rearrange("p t (h a c) -> p a t h c", a=2, c=ROPE)
            nc.vector.tensor_tensor(
                out=o4[:, t0 + lo : t0 + lo + n, hs, 1 + NOPE : HEAD_OUT],
                in0=mv[:, 0, lo : lo + n, :, :],
                in1=rb[:, lo : lo + n, 512 * quad : 512 * (quad + 1)].rearrange("p t (h c) -> p t h c", c=ROPE),
                op=ALU.add,
            )
            for t in range(t0 + lo, t0 + lo + n):
                mark(t, quad)

        def add_rb_gpsimd(mpair, quad, t0, s):
            hs = slice(4 * quad, 4 * quad + 4)
            mv = mpair.rearrange("p t (h a c) -> p a t h c", a=2, c=ROPE)
            nc.gpsimd.tensor_tensor(
                out=o4[:, t0 + s, hs, 1 + NOPE : HEAD_OUT],
                in0=mv[:, 0, s, :, :],
                in1=rb[:, s, 512 * quad : 512 * (quad + 1)].rearrange("p (h c) -> p h c", c=ROPE),
                op=ALU.add,
            )
            mark(t0 + s, quad)

        def emit_r(n):
            for unused in range(n):
                if r_pos[0] < len(r_units):
                    r_units[r_pos[0]]()
                    r_pos[0] += 1

        emit_load(0, (0,))
        nc.vector.memset(bt.bitcast(I32), 0)
        nc.vector.memset(zrhs.bitcast(I32), 0)
        nc.vector.memset(one_col[:, :], 1.0)
        make_identity(nc, ident[:, :])
        nc.sync.dma_start(out=bt[0:HEADS, :], in_=wq_b.rearrange("(h r) -> h r", r=QK)[:, NOPE:QK])
        nc.sync.dma_start(out=cs[:, :, 0, :], in_=cos_src)
        nc.sync.dma_start(out=cs[:, :, 1, :], in_=sin_src)
        emit_load(0, (1, 2, 3))
        nc.scalar.activation(out=scr_col[:, :], in_=one_col[:, :], func=ACT.Sqrt)
        for i in range(1, RAW_BUFS):
            emit_load(i)
        nc.sync.dma_start(out=b_all[:, :], in_=wq_b.partition_broadcast(P))

        nc.vector.tensor_copy(out=ident_b[:, :], in_=ident[:, :])
        emit_dummies(WARMUP)
        nc.vector.tensor_copy(
            out=perm.rearrange("p (e j) -> p e j", e=2), in_=ident.rearrange("p (j e) -> p e j", e=2)
        )
        nc.vector.tensor_tensor(out=eye2[:, :], in0=ident[:, 0:64], in1=ident[:, 64:128], op=ALU.add)

        def emit_tables():
            bt_je = bt.rearrange("p (j e) -> p e j", e=2)
            nc.gpsimd.tensor_copy(out=bt2[:, 0, 0:64], in_=bt_je[:, 0, :])
            nc.gpsimd.tensor_scalar(
                out=bt2[:, 0, 64:128], in0=bt_je[:, 1, :], scalar1=-1.0, scalar2=0.0, op0=ALU.mult, op1=ALU.add
            )
            nc.gpsimd.tensor_copy(out=bt2[:, 1, 0:64], in_=bt_je[:, 1, :])
            nc.gpsimd.tensor_copy(out=bt2[:, 1, 64:128], in_=bt_je[:, 0, :])
            small = ps_tr.tile([P, 4, P], BF16, name="trb", tag="trb")
            for st in range(2):
                nc.tensor.transpose(small[:, st, :], cs[:, st, :, :].rearrange("p a j -> p (a j)"), ident_b[:, :])
            for e in range(2):
                nc.tensor.transpose(small[:, 2 + e, :], bt2[:, e, :], ident_b[:, :])
            nc.scalar.copy(out=cs_t[:, :, :], in_=small[:, 0:2, :])
            nc.scalar.copy(out=coef[:, :, :], in_=small[:, 2:4, 0:HEADS].rearrange("p e h -> p h e"))
            for quad in range(4):
                nc.gpsimd.tensor_tensor(
                    out=dmat[:, 512 * quad : 512 * (quad + 1)].rearrange("p (h j e) -> p h j e", j=64, e=2),
                    in0=eye2[:, :].unsqueeze(1).unsqueeze(3).to_broadcast([P, 4, 64, 2]),
                    in1=coef[:, 4 * quad : 4 * quad + 4, :].unsqueeze(2).to_broadcast([P, 4, 64, 2]),
                    op=ALU.mult,
                )
            nc.vector.tensor_copy(out=tab1[:, :, 0, :, 0], in_=cs[:, :, 0, :])
            nc.vector.tensor_copy(out=tab1[:, :, 0, :, 1], in_=cs[:, :, 1, :])
            nc.vector.tensor_scalar_mul(out=tab1[:, :, 1, :, 0], in0=cs[:, :, 1, :], scalar1=-1.0)
            nc.vector.tensor_copy(out=tab1[:, :, 1, :, 1], in_=cs[:, :, 0, :])
            nc.vector.tensor_copy(
                out=tabf[:, :, :, :],
                in_=tab1.rearrange("p s a j e -> p s (a j e)").unsqueeze(2).to_broadcast([P, 2, 4, 256]),
            )

        emit_tables()
        emit_run(0, V_EVAC["H"])
        emit_quant(0)
        emit_run(1, V_EVAC["H"])
        emit_rb(0)
        emit_quant(1)
        emit_run(2, V_EVAC["H"])
        emit_rb(1)
        emit_quant(2)
        emit_run(3, V_EVAC["H"])

        n_steps = 2 * len(CHUNKS)
        for step in range(n_steps):
            c = step // 2
            hf = step % 2
            kind, idx = CHUNKS[c]
            runs = RUNS_BEFORE_STEP.get(step, (step + 4,))
            todo = [i for i in runs if i < N_RUNS]
            for n, i in enumerate(todo):
                if n > 0:
                    emit_rb(2)
                emit_run(i, V_EVAC[kind])
            flush_scalar(QUADS_PER_FLUSH)
            emit_r(UNITS_BEFORE[kind])
            for n, i in enumerate(todo):
                if n > 0:
                    emit_r(2)
                emit_quant(i)
            if kind == "P":
                mpair = mpool.tile([P, 2, 1024], F32, name="mpair", tag="mpair")
            for t2 in range(2):
                tt = 2 * hf + t2
                acc = emit_mx(c, tt)
                if kind == "P":
                    products(acc, tt, mpair)
                else:
                    evac_nope(acc, idx, tt)
                emit_r(UNITS_AFTER[kind][t2])
            if kind == "P" and step < n_steps - 2:
                r_units.append(lambda mp=mpair: sum_products(mp, 0, 2))
                r_units.append(lambda mp=mpair, q=idx, t=2 * hf: add_rb(mp, q, t, 0, 2))
            if step == n_steps - 2:
                emit_r(len(r_units))
                sum_products(mpair, 0, 2)
                for s in range(2):
                    add_rb_gpsimd(mpair, idx, 2 * hf, s)
            if step == n_steps - 1:
                for s in range(2):
                    r_units.append(lambda mp=mpair, s=s: sum_products(mp, s, 1))
                for s in range(2):
                    r_units.append(lambda mp=mpair, q=idx, t=2 * hf, s=s: add_rb(mp, q, t, s, 1))
            if step == 0:
                emit_quant(3)
            if step == 3:
                emit_rb(3)
        while r_pos[0] < len(r_units):
            emit_r(1)
            flush_scalar(2)
        flush_scalar(4)
